import numpy as np
import ml_dtypes


def mxq(x, axis, fmt="e4m3"):
    dtype, down = {"e4m3": (ml_dtypes.float8_e4m3fn, 7), "e5m2": (ml_dtypes.float8_e5m2, 14)}[fmt]
    v = np.moveaxis(np.asarray(x, np.float32).astype(ml_dtypes.bfloat16).astype(np.float64), axis, -1)
    blocks = v.reshape(v.shape[:-1] + (-1, 32))
    amax = np.abs(blocks).max(-1, keepdims=True)
    byte = np.maximum(np.where(amax > 0, np.frexp(amax)[1] - 1 + 127, 0) - down, 1)
    scale = np.exp2(byte - 127.0)
    codes = (blocks / scale).astype(np.float32).astype(dtype).astype(np.float64)
    return np.moveaxis((codes * scale).reshape(v.shape), -1, axis)


WIDE = False


def mx_kscale(k):
    if not WIDE:
        return np.ones(k)
    levels = np.array([10, -10, 5, -5, 0])
    a = np.random.permutation(np.resize(levels, k // 512 * 4)).reshape(k // 512, 4)
    idx = np.arange(k)
    return np.exp2(a[idx // 512, idx % 128 // 32])


BF16 = ml_dtypes.bfloat16


def bf(x):
    return np.asarray(x, np.float32).astype(BF16)


def f64(x):
    return np.asarray(x).astype(np.float64)


E2M1 = np.array([0.0, 0.5, 1.0, 1.5, 2.0, 3.0, 4.0, 6.0, -0.0, -0.5, -1.0, -1.5, -2.0, -3.0, -4.0, -6.0])


def pack_weight(w, fmt):
    k, n = w.shape
    w = f64(bf(w)).reshape(k // 32, 32, n)
    amax = np.abs(w).max(1)
    if fmt == "e4m3":
        byte = np.frexp(amax)[1] - 1 + 127 - 7
    else:
        mant, ex = np.frexp(amax / 6.0)
        byte = np.where(mant > 0.5, ex, ex - 1) + 127
    byte = np.clip(np.where(amax > 0, byte, 1), 1, 254)
    scaled = (w * np.exp2(127.0 - byte)[:, None, :]).reshape(k, n).astype(np.float32)
    by_word = np.ascontiguousarray(scaled.reshape(k // 512, 128, 4, n).transpose(0, 1, 3, 2))
    if fmt == "e4m3":
        words = by_word.astype(ml_dtypes.float8_e4m3fn).view(np.uint8)
    else:
        c = by_word.astype(ml_dtypes.float4_e2m1fn).view(np.uint8) & 0xF
        words = c[..., 0::2] | (c[..., 1::2] << 4)
    return np.ascontiguousarray(words), np.ascontiguousarray(byte.astype(np.uint8).reshape(k // 512, 16, n))


def unpack_weight(words, scales, fmt):
    g, p, n, _ = words.shape
    if fmt == "e4m3":
        vals = np.ascontiguousarray(words).view(ml_dtypes.float8_e4m3fn).astype(np.float64)
    else:
        nib = np.empty((g, p, n, 4), np.uint8)
        nib[..., 0::2] = words & 0xF
        nib[..., 1::2] = words >> 4
        vals = E2M1[nib]
    vals = vals * np.repeat(np.exp2(scales.astype(np.float64) - 127.0), 8, axis=1)[..., None]
    return vals.transpose(0, 1, 3, 2).reshape(g * 512, n)


B, I, H = 4096, 512, 512
EPS = 1e-5
FMT = "e4m3"


def sigmoid(v):
    return 1.0 / (1.0 + np.exp(-v))


def ln(v, g, b):
    m = v.mean(-1, keepdims=True)
    var = np.square(v - m).mean(-1, keepdims=True)
    return (v - m) / np.sqrt(var + EPS) * g + b


def setup_inputs():
    s, t = mx_kscale(I), mx_kscale(H)
    d = {"x": bf(np.random.standard_normal((B, I)) * s), "h": bf(np.random.standard_normal((B, H)) * t),
         "c": bf(np.random.standard_normal((B, H))), "ic_tilde": bf(0.35 * np.random.standard_normal((B, H)))}
    for g in ("f", "o"):
        w = np.random.standard_normal((H, I)) / np.sqrt(I) / s[None, :]
        words, scales = pack_weight(np.ascontiguousarray(w.T), FMT)
        d["W" + g + "_w_words"] = words
        d["W" + g + "_w_scales"] = scales
        d["W" + g + "_b"] = bf(np.random.standard_normal(H) * 0.5)
        u = np.random.standard_normal((H, H)) / np.sqrt(H) / t[None, :]
        words, scales = pack_weight(np.ascontiguousarray(u.T), FMT)
        d["U" + g + "_w_words"] = words
        d["U" + g + "_w_scales"] = scales
        d["ln" + g + "_g"] = bf(1.0 + 0.2 * np.random.standard_normal(H))
        d["ln" + g + "_b"] = bf(0.2 * np.random.standard_normal(H))
    return d


def reference(x, h, c, ic_tilde, Wf_w_words, Wf_w_scales, Wf_b, Uf_w_words, Uf_w_scales, lnf_g, lnf_b,
              Wo_w_words, Wo_w_scales, Wo_b, Uo_w_words, Uo_w_scales, lno_g, lno_b):
    xq = mxq(f64(x), 1, "e4m3")
    hq = mxq(f64(h), 1, "e4m3")
    pre_f = (xq @ unpack_weight(Wf_w_words, Wf_w_scales, FMT)) + f64(Wf_b) + (hq @ unpack_weight(Uf_w_words, Uf_w_scales, FMT))
    pre_o = (xq @ unpack_weight(Wo_w_words, Wo_w_scales, FMT)) + f64(Wo_b) + (hq @ unpack_weight(Uo_w_words, Uo_w_scales, FMT))
    f = sigmoid(ln(pre_f, f64(lnf_g), f64(lnf_b)))
    o = sigmoid(ln(pre_o, f64(lno_g), f64(lno_b)))
    c_new = f * f64(c) + f64(ic_tilde)
    h_new = o * np.tanh(c_new)
    return (h_new, c_new)

@@ -1,0 +1,169 @@
+from contextlib import ExitStack
+
+import concourse.mybir as mybir
+from concourse.masks import make_identity
+
+F32 = mybir.dt.float32
+BF16 = mybir.dt.bfloat16
+I32 = mybir.dt.int32
+U8 = mybir.dt.uint8
+U32 = mybir.dt.uint32
+FP8X4 = mybir.dt.float8_e4m3fn_x4
+ALU = mybir.AluOpType
+ACT = mybir.ActivationFunctionType
+
+P = 128
+ROWS = 4096
+FEATURES = 512
+ROW_TILES = ROWS // P
+GROUP = 4
+WORDS = FEATURES // 2
+EPS = 1e-5
+FLOPS = 4 * 2 * ROWS * FEATURES * FEATURES
+
+FORGET, OUTPUT = 0, 1
+
+
+def tile_layernormlstmcell_pb_t_kernel(
+    tc, x, h, c, ic_tilde,
+    Wf_w_words, Wf_w_scales, Wf_b, Uf_w_words, Uf_w_scales, lnf_g, lnf_b,
+    Wo_w_words, Wo_w_scales, Wo_b, Uo_w_words, Uo_w_scales, lno_g, lno_b,
+    out_0, out_1,
+):
+    nc = tc.nc
+    x_rows = x.rearrange("(p t) k -> p t k", t=ROW_TILES)
+    h_rows = h.rearrange("(p t) k -> p t k", t=ROW_TILES)
+    c_rows = c.rearrange("(p t) k -> p t k", t=ROW_TILES)
+    ic_rows = ic_tilde.rearrange("(p t) k -> p t k", t=ROW_TILES)
+    h_new_rows = out_0.rearrange("(p t) k -> p t k", t=ROW_TILES)
+    c_new_rows = out_1.rearrange("(p t) k -> p t k", t=ROW_TILES)
+
+    with ExitStack() as ctx:
+        const = ctx.enter_context(tc.tile_pool(name="const", bufs=1))
+        loads = ctx.enter_context(tc.tile_pool(name="loads", bufs=3))
+        stores = ctx.enter_context(tc.tile_pool(name="stores", bufs=2))
+        work = ctx.enter_context(tc.tile_pool(name="work", bufs=3))
+        small = ctx.enter_context(tc.tile_pool(name="small", bufs=4))
+        psum_t = ctx.enter_context(tc.psum_pool(name="psum_t", bufs=2))
+        psum_acc = ctx.enter_context(tc.psum_pool(name="psum_acc", bufs=2))
+
+        ident = const.tile([P, P], F32)
+        make_identity(nc, ident[:])
+        neg_half = const.tile([P, 2], F32)
+        nc.vector.memset(neg_half[:], -0.5)
+
+        weights = ((Wf_w_words, Wf_w_scales), (Uf_w_words, Uf_w_scales),
+                   (Wo_w_words, Wo_w_scales), (Uo_w_words, Uo_w_scales))
+        w_codes = const.tile([P, 4, 4 * FEATURES], U8, align_bytes=64)
+        w_scales = const.tile([P, 4, FEATURES], U8, align_bytes=64)
+        nc.vector.memset(w_scales[:].bitcast(I32), 0)
+        for w, (words, scales) in enumerate(weights):
+            for quadrant in range(4):
+                nc.sync.dma_start(
+                    out=w_scales[32 * quadrant : 32 * quadrant + 4, w, :].bitcast(I32),
+                    in_=scales[0, 4 * quadrant : 4 * quadrant + 4, :].bitcast(I32),
+                )
+        for w, (words, scales) in enumerate(weights):
+            nc.sync.dma_start(
+                out=w_codes[:, w, :].bitcast(I32),
+                in_=words.rearrange("g p n t -> (g p) (n t)").bitcast(I32),
+            )
+
+        bias = const.tile([P, 2, FEATURES], BF16)
+        gain = const.tile([P, 2, FEATURES], BF16)
+        shift = const.tile([P, 2, FEATURES], BF16)
+        for gate, (b_vec, g_vec, s_vec) in enumerate(((Wf_b, lnf_g, lnf_b), (Wo_b, lno_g, lno_b))):
+            nc.scalar.dma_start(out=bias[:, gate, :], in_=b_vec.partition_broadcast(P))
+            nc.scalar.dma_start(out=gain[:, gate, :], in_=g_vec.partition_broadcast(P))
+            nc.scalar.dma_start(out=shift[:, gate, :], in_=s_vec.partition_broadcast(P))
+
+        for first in range(0, ROW_TILES, GROUP):
+            tiles = slice(first, first + GROUP)
+            x_sb = loads.tile([P, GROUP, FEATURES], BF16)
+            h_sb = loads.tile([P, GROUP, FEATURES], BF16)
+            c_sb = loads.tile([P, GROUP, FEATURES], BF16)
+            ic_sb = loads.tile([P, GROUP, FEATURES], BF16)
+            nc.sync.dma_start(out=x_sb[:], in_=x_rows[:, tiles, :])
+            nc.sync.dma_start(out=h_sb[:], in_=h_rows[:, tiles, :])
+            nc.sync.dma_start(out=c_sb[:], in_=c_rows[:, tiles, :])
+            nc.sync.dma_start(out=ic_sb[:], in_=ic_rows[:, tiles, :])
+            c_new = stores.tile([P, GROUP, FEATURES], F32)
+            h_new = stores.tile([P, GROUP, FEATURES], F32)
+
+            for i in range(GROUP):
+                turned = psum_t.tile([P, 2, 2, P], F32)
+                for a, source in enumerate((x_sb, h_sb)):
+                    words = source[:, i, :].bitcast(F32)
+                    for u in range(2):
+                        nc.tensor.transpose(turned[:, a, u, :], words[:, u:WORDS:2], ident[:])
+                grouped = work.tile([P, 2, P, 4], BF16, align_bytes=64)
+                nc.scalar.copy(out=grouped[:].bitcast(F32), in_=turned[:].rearrange("p a u r -> p a r u"))
+                xh_codes = work.tile([P, 2 * P], U32, align_bytes=64)
+                xh_scales = work.tile([P, 2 * P], U8, align_bytes=64)
+                nc.vector.quantize_mx(
+                    out=xh_codes[:].bitcast(FP8X4),
+                    scales=xh_scales[:],
+                    in_=grouped[:].rearrange("p a r t -> p (a r t)"),
+                )
+
+                pre = [psum_acc.tile([P, FEATURES], F32, name="pre_f"),
+                       psum_acc.tile([P, FEATURES], F32, name="pre_o")]
+                for a in range(2):
+                    for gate in range(2):
+                        w = 2 * gate + a
+                        nc.tensor.matmul_mx(
+                            out=pre[gate][:],
+                            lhsT=xh_codes[:, a * P : (a + 1) * P].bitcast(FP8X4),
+                            lhsT_scale=xh_scales[:, a * P : (a + 1) * P],
+                            rhs=w_codes[:, w, :].bitcast(FP8X4),
+                            rhs_scale=w_scales[:, w, :],
+                            start=(a == 0),
+                            stop=(a == 1),
+                        )
+
+                y = [work.tile([P, FEATURES], F32, name="y_f"), work.tile([P, FEATURES], F32, name="y_o")]
+                row_sum = small.tile([P, 2], F32)
+                for gate in range(2):
+                    nc.vector.scalar_tensor_tensor(
+                        out=y[gate][:], in0=pre[gate][:], scalar=1.0, in1=bias[:, gate, :],
+                        op0=ALU.mult, op1=ALU.add, accum_out=row_sum[:, gate : gate + 1],
+                    )
+                neg_mean = small.tile([P, 2], F32)
+                nc.gpsimd.tensor_scalar(out=neg_mean[:], in0=row_sum[:], scalar1=-1.0 / FEATURES,
+                                        scalar2=0.0, op0=ALU.mult, op1=ALU.add)
+                sum_sq = small.tile([P, 2], F32)
+                for gate in range(2):
+                    squares = work.tile([P, FEATURES], BF16)
+                    nc.scalar.activation(
+                        out=squares[:], in_=y[gate][:], func=ACT.Square,
+                        bias=neg_mean[:, gate : gate + 1], scale=1.0,
+                        accum_out=sum_sq[:, gate : gate + 1],
+                    )
+                var_eps = small.tile([P, 2], F32)
+                nc.gpsimd.tensor_scalar(out=var_eps[:], in0=sum_sq[:], scalar1=1.0 / FEATURES,
+                                        scalar2=EPS, op0=ALU.mult, op1=ALU.add)
+                rstd = small.tile([P, 2], F32)
+                nc.gpsimd.tensor_tensor(out=rstd[:], in0=var_eps[:], in1=neg_half[:], op=ALU.pow)
+
+                gates = [work.tile([P, FEATURES], F32, name="gate_f"),
+                         work.tile([P, FEATURES], F32, name="gate_o")]
+                for gate in range(2):
+                    nc.vector.scalar_tensor_tensor(
+                        out=gates[gate][:], in0=y[gate][:], scalar=neg_mean[:, gate : gate + 1],
+                        in1=gain[:, gate, :], op0=ALU.add, op1=ALU.mult,
+                    )
+                    nc.vector.scalar_tensor_tensor(
+                        out=gates[gate][:], in0=gates[gate][:], scalar=rstd[:, gate : gate + 1],
+                        in1=shift[:, gate, :], op0=ALU.mult, op1=ALU.add,
+                    )
+                    nc.scalar.activation(out=gates[gate][:], in_=gates[gate][:], func=ACT.Sigmoid)
+
+                kept = work.tile([P, FEATURES], F32)
+                nc.vector.tensor_tensor(out=kept[:], in0=gates[FORGET][:], in1=c_sb[:, i, :], op=ALU.mult)
+                nc.vector.tensor_tensor(out=c_new[:, i, :], in0=kept[:], in1=ic_sb[:, i, :], op=ALU.add)
+                squashed = work.tile([P, FEATURES], F32)
+                nc.scalar.activation(out=squashed[:], in_=c_new[:, i, :], func=ACT.Tanh)
+                nc.vector.tensor_tensor(out=h_new[:, i, :], in0=gates[OUTPUT][:], in1=squashed[:], op=ALU.mult)
+
+            nc.sync.dma_start(out=c_new_rows[:, tiles, :], in_=c_new[:])
+            nc.sync.dma_start(out=h_new_rows[:, tiles, :], in_=h_new[:])

@@ -16,12 +16,27 @@ P = 128
 ROWS = 4096
 FEATURES = 512
 ROW_TILES = ROWS // P
-GROUP = 4
+BLOCKS = FEATURES // P
+CHUNK = 4
+CHUNKS = ROW_TILES // CHUNK
+BLOCKS_A_STEP = BLOCKS // CHUNK
 WORDS = FEATURES // 2
 EPS = 1e-5
 FLOPS = 4 * 2 * ROWS * FEATURES * FEATURES
 
 FORGET, OUTPUT = 0, 1
+
+LAG_QUANTISE = 1
+LAG_PRODUCT = 2
+LAG_BIAS = 3
+LAG_SQUARES = 4
+LAG_NORMALISE = 5
+LAG_GATE = LAG_NORMALISE + CHUNK
+LAG_BACK_F = LAG_GATE + CHUNK
+LAG_KEEP = LAG_BACK_F + 1
+LAG_TANH = LAG_KEEP + 1
+LAG_BACK_O = LAG_TANH
+LAG_OUT = LAG_BACK_O + 1
 
 
 def tile_layernormlstmcell_pb_t_kernel(
@@ -40,130 +55,243 @@ def tile_layernormlstmcell_pb_t_kernel(
 
     with ExitStack() as ctx:
         const = ctx.enter_context(tc.tile_pool(name="const", bufs=1))
-        loads = ctx.enter_context(tc.tile_pool(name="loads", bufs=3))
+        loads = ctx.enter_context(tc.tile_pool(name="loads", bufs=2))
         stores = ctx.enter_context(tc.tile_pool(name="stores", bufs=2))
         work = ctx.enter_context(tc.tile_pool(name="work", bufs=3))
+        chunks = ctx.enter_context(tc.tile_pool(name="chunks", bufs=2))
         small = ctx.enter_context(tc.tile_pool(name="small", bufs=4))
-        psum_t = ctx.enter_context(tc.psum_pool(name="psum_t", bufs=2))
-        psum_acc = ctx.enter_context(tc.psum_pool(name="psum_acc", bufs=2))
+        psum = ctx.enter_context(tc.psum_pool(name="psum", bufs=1))
+        ctx.enter_context(tc.manual_schedule())
 
-        ident = const.tile([P, P], F32)
-        make_identity(nc, ident[:])
-        neg_half = const.tile([P, 2], F32)
-        nc.vector.memset(neg_half[:], -0.5)
+        x_sb, h_sb, c_sb, ic_sb, c_new, h_new = {}, {}, {}, {}, {}, {}
+        grouped, xh_codes, xh_scales, pre, y = {}, {}, {}, {}, {}
+        neg_mean, rstd, normed, gate_t, back, kept, squashed = {}, {}, {}, {}, {}, {}, {}
+
+        def chunk_tiles(k):
+            return slice(k * CHUNK, (k + 1) * CHUNK)
+
+        def load_x_h(k):
+            x_sb[k] = loads.tile([P, CHUNK, FEATURES], BF16, name="x_sb")
+            h_sb[k] = loads.tile([P, CHUNK, FEATURES], BF16, name="h_sb")
+            nc.sync.dma_start(out=x_sb[k][:], in_=x_rows[:, chunk_tiles(k), :])
+            nc.sync.dma_start(out=h_sb[k][:], in_=h_rows[:, chunk_tiles(k), :])
+
+        def load_c_ic(k):
+            c_sb[k] = loads.tile([P, CHUNK, FEATURES], BF16, name="c_sb")
+            ic_sb[k] = loads.tile([P, CHUNK, FEATURES], BF16, name="ic_sb")
+            nc.sync.dma_start(out=c_sb[k][:], in_=c_rows[:, chunk_tiles(k), :])
+            nc.sync.dma_start(out=ic_sb[k][:], in_=ic_rows[:, chunk_tiles(k), :])
+
+        load_x_h(0)
 
         weights = ((Wf_w_words, Wf_w_scales), (Uf_w_words, Uf_w_scales),
                    (Wo_w_words, Wo_w_scales), (Uo_w_words, Uo_w_scales))
         w_codes = const.tile([P, 4, 4 * FEATURES], U8, align_bytes=64)
         w_scales = const.tile([P, 4, FEATURES], U8, align_bytes=64)
         nc.vector.memset(w_scales[:].bitcast(I32), 0)
-        for w, (words, scales) in enumerate(weights):
+        for w, (code_bytes, scale_bytes) in enumerate(weights):
             for quadrant in range(4):
                 nc.sync.dma_start(
                     out=w_scales[32 * quadrant : 32 * quadrant + 4, w, :].bitcast(I32),
-                    in_=scales[0, 4 * quadrant : 4 * quadrant + 4, :].bitcast(I32),
+                    in_=scale_bytes[0, 4 * quadrant : 4 * quadrant + 4, :].bitcast(I32),
                 )
-        for w, (words, scales) in enumerate(weights):
+        for w, (code_bytes, scale_bytes) in enumerate(weights):
             nc.sync.dma_start(
                 out=w_codes[:, w, :].bitcast(I32),
-                in_=words.rearrange("g p n t -> (g p) (n t)").bitcast(I32),
+                in_=code_bytes.rearrange("g p n t -> (g p) (n t)").bitcast(I32),
             )
 
+        ident = const.tile([P, P], F32)
+        make_identity(nc, ident[:])
+        ident_bf = const.tile([P, P], BF16)
+        make_identity(nc, ident_bf[:])
+        neg_half = const.tile([P, 2], F32)
+        nc.vector.memset(neg_half[:], -0.5)
+
+        vectors = const.tile([P, FEATURES], BF16)
+        nc.vector.memset(vectors[:], 0.0)
+        for v, vector in enumerate((lnf_g, lnf_b, lno_g, lno_b, Wf_b, Wo_b)):
+            nc.scalar.dma_start(out=vectors[v : v + 1, :], in_=vector.unsqueeze(0))
+        columns = psum.tile([P, BLOCKS, P], BF16, name="columns", tag="turned")
+        for j in range(BLOCKS):
+            nc.tensor.transpose(columns[:, j, :], vectors[:, j * P : (j + 1) * P], ident_bf[:])
+        affine = const.tile([P, BLOCKS, 4], F32)
+        nc.vector.tensor_copy(out=affine[:], in_=columns[:, :, 0:4])
         bias = const.tile([P, 2, FEATURES], BF16)
-        gain = const.tile([P, 2, FEATURES], BF16)
-        shift = const.tile([P, 2, FEATURES], BF16)
-        for gate, (b_vec, g_vec, s_vec) in enumerate(((Wf_b, lnf_g, lnf_b), (Wo_b, lno_g, lno_b))):
-            nc.scalar.dma_start(out=bias[:, gate, :], in_=b_vec.partition_broadcast(P))
-            nc.scalar.dma_start(out=gain[:, gate, :], in_=g_vec.partition_broadcast(P))
-            nc.scalar.dma_start(out=shift[:, gate, :], in_=s_vec.partition_broadcast(P))
+        for gate in range(2):
+            spread = psum.tile([P, FEATURES], F32, name="spread", tag="pre", bufs=3)
+            nc.tensor.matmul(spread[:], lhsT=ident_bf[:, 4 + gate : 5 + gate].to_broadcast([P, P]),
+                             rhs=vectors[:], start=True, stop=True)
+            nc.vector.tensor_copy(out=bias[:, gate, :], in_=spread[:])
 
-        for first in range(0, ROW_TILES, GROUP):
-            tiles = slice(first, first + GROUP)
-            x_sb = loads.tile([P, GROUP, FEATURES], BF16)
-            h_sb = loads.tile([P, GROUP, FEATURES], BF16)
-            c_sb = loads.tile([P, GROUP, FEATURES], BF16)
-            ic_sb = loads.tile([P, GROUP, FEATURES], BF16)
-            nc.sync.dma_start(out=x_sb[:], in_=x_rows[:, tiles, :])
-            nc.sync.dma_start(out=h_sb[:], in_=h_rows[:, tiles, :])
-            nc.sync.dma_start(out=c_sb[:], in_=c_rows[:, tiles, :])
-            nc.sync.dma_start(out=ic_sb[:], in_=ic_rows[:, tiles, :])
-            c_new = stores.tile([P, GROUP, FEATURES], F32)
-            h_new = stores.tile([P, GROUP, FEATURES], F32)
+        def turn(t):
+            k, i = divmod(t, CHUNK)
+            turned = psum.tile([P, 2, 2, P], F32, name="turned")
+            for a, source in enumerate((x_sb[k], h_sb[k])):
+                pairs = source[:, i, :].bitcast(F32)
+                for u in range(2):
+                    nc.tensor.transpose(turned[:, a, u, :], pairs[:, u:WORDS:2], ident[:])
+            grouped[t] = work.tile([P, 2, P, 4], BF16, name="grouped", align_bytes=64)
+            side_by_side = turned[:].rearrange("p a u r -> p a r u")
+            if t % 2 == 0:
+                nc.scalar.copy(out=grouped[t][:].bitcast(F32), in_=side_by_side)
+            else:
+                nc.vector.tensor_copy(out=grouped[t][:].bitcast(F32), in_=side_by_side)
 
-            for i in range(GROUP):
-                turned = psum_t.tile([P, 2, 2, P], F32)
-                for a, source in enumerate((x_sb, h_sb)):
-                    words = source[:, i, :].bitcast(F32)
-                    for u in range(2):
-                        nc.tensor.transpose(turned[:, a, u, :], words[:, u:WORDS:2], ident[:])
-                grouped = work.tile([P, 2, P, 4], BF16, align_bytes=64)
-                nc.scalar.copy(out=grouped[:].bitcast(F32), in_=turned[:].rearrange("p a u r -> p a r u"))
-                xh_codes = work.tile([P, 2 * P], U32, align_bytes=64)
-                xh_scales = work.tile([P, 2 * P], U8, align_bytes=64)
-                nc.vector.quantize_mx(
-                    out=xh_codes[:].bitcast(FP8X4),
-                    scales=xh_scales[:],
-                    in_=grouped[:].rearrange("p a r t -> p (a r t)"),
+        def quantise(t):
+            xh_codes[t] = work.tile([P, 2 * P], U32, name="xh_codes", align_bytes=64)
+            xh_scales[t] = work.tile([P, 2 * P], U8, name="xh_scales", align_bytes=64)
+            nc.vector.quantize_mx(
+                out=xh_codes[t][:].bitcast(FP8X4),
+                scales=xh_scales[t][:],
+                in_=grouped[t][:].rearrange("p a r t -> p (a r t)"),
+            )
+
+        def products(t):
+            pre[t] = [psum.tile([P, FEATURES], F32, name="pre_f", tag="pre", bufs=3),
+                      psum.tile([P, FEATURES], F32, name="pre_o", tag="pre", bufs=3)]
+            for a in range(2):
+                for gate in range(2):
+                    w = 2 * gate + a
+                    nc.tensor.matmul_mx(
+                        out=pre[t][gate][:],
+                        lhsT=xh_codes[t][:, a * P : (a + 1) * P].bitcast(FP8X4),
+                        lhsT_scale=xh_scales[t][:, a * P : (a + 1) * P],
+                        rhs=w_codes[:, w, :].bitcast(FP8X4),
+                        rhs_scale=w_scales[:, w, :],
+                        start=(a == 0),
+                        stop=(a == 1),
+                    )
+
+        def add_bias(t):
+            y[t] = [work.tile([P, FEATURES], F32, name="y_f", bufs=4),
+                    work.tile([P, FEATURES], F32, name="y_o", bufs=4)]
+            row_sum = small.tile([P, 2], F32, name="row_sum")
+            for gate in range(2):
+                nc.vector.scalar_tensor_tensor(
+                    out=y[t][gate][:], in0=pre[t][gate][:], scalar=1.0, in1=bias[:, gate, :],
+                    op0=ALU.mult, op1=ALU.add, accum_out=row_sum[:, gate : gate + 1],
                 )
+            neg_mean[t] = small.tile([P, 2], F32, name="neg_mean")
+            nc.vector.tensor_scalar_mul(out=neg_mean[t][:], in0=row_sum[:], scalar1=-1.0 / FEATURES)
 
-                pre = [psum_acc.tile([P, FEATURES], F32, name="pre_f"),
-                       psum_acc.tile([P, FEATURES], F32, name="pre_o")]
-                for a in range(2):
-                    for gate in range(2):
-                        w = 2 * gate + a
-                        nc.tensor.matmul_mx(
-                            out=pre[gate][:],
-                            lhsT=xh_codes[:, a * P : (a + 1) * P].bitcast(FP8X4),
-                            lhsT_scale=xh_scales[:, a * P : (a + 1) * P],
-                            rhs=w_codes[:, w, :].bitcast(FP8X4),
-                            rhs_scale=w_scales[:, w, :],
-                            start=(a == 0),
-                            stop=(a == 1),
-                        )
+        def squares(t):
+            sum_sq = small.tile([P, 2], F32, name="sum_sq")
+            for gate in range(2):
+                unused = work.tile([P, FEATURES], BF16, name="unused")
+                nc.scalar.activation(
+                    out=unused[:], in_=y[t][gate][:], func=ACT.Square,
+                    bias=neg_mean[t][:, gate : gate + 1], scale=1.0,
+                    accum_out=sum_sq[:, gate : gate + 1],
+                )
+            var_eps = small.tile([P, 2], F32, name="var_eps")
+            nc.gpsimd.tensor_scalar(out=var_eps[:], in0=sum_sq[:], scalar1=1.0 / FEATURES,
+                                    scalar2=EPS, op0=ALU.mult, op1=ALU.add)
+            rstd[t] = small.tile([P, 2], F32, name="rstd")
+            nc.gpsimd.tensor_tensor(out=rstd[t][:], in0=var_eps[:], in1=neg_half[:], op=ALU.pow)
 
-                y = [work.tile([P, FEATURES], F32, name="y_f"), work.tile([P, FEATURES], F32, name="y_o")]
-                row_sum = small.tile([P, 2], F32)
-                for gate in range(2):
-                    nc.vector.scalar_tensor_tensor(
-                        out=y[gate][:], in0=pre[gate][:], scalar=1.0, in1=bias[:, gate, :],
-                        op0=ALU.mult, op1=ALU.add, accum_out=row_sum[:, gate : gate + 1],
-                    )
-                neg_mean = small.tile([P, 2], F32)
-                nc.gpsimd.tensor_scalar(out=neg_mean[:], in0=row_sum[:], scalar1=-1.0 / FEATURES,
-                                        scalar2=0.0, op0=ALU.mult, op1=ALU.add)
-                sum_sq = small.tile([P, 2], F32)
-                for gate in range(2):
-                    squares = work.tile([P, FEATURES], BF16)
+        def normalise(t):
+            k, i = divmod(t, CHUNK)
+            if i == 0:
+                normed[k] = [chunks.tile([P, CHUNK, FEATURES], F32, name="normed_f"),
+                             chunks.tile([P, CHUNK, FEATURES], F32, name="normed_o")]
+            nc.gpsimd.tensor_scalar(
+                out=normed[k][FORGET][:, i, :], in0=y[t][FORGET][:],
+                scalar1=neg_mean[t][:, FORGET : FORGET + 1], scalar2=rstd[t][:, FORGET : FORGET + 1],
+                op0=ALU.add, op1=ALU.mult,
+            )
+            nc.vector.tensor_scalar(
+                out=normed[k][OUTPUT][:, i, :], in0=y[t][OUTPUT][:],
+                scalar1=neg_mean[t][:, OUTPUT : OUTPUT + 1], scalar2=rstd[t][:, OUTPUT : OUTPUT + 1],
+                op0=ALU.add, op1=ALU.mult,
+            )
+
+        def gates(unit):
+            k, part = divmod(unit, CHUNK)
+            if part == 0:
+                gate_t[k] = [chunks.tile([P, BLOCKS, CHUNK * P], F32, name="gate_t_f"),
+                             chunks.tile([P, BLOCKS, CHUNK * P], F32, name="gate_t_o", bufs=3)]
+            blocks = range(part * BLOCKS_A_STEP, (part + 1) * BLOCKS_A_STEP)
+            normed_t = [psum.tile([P, BLOCKS_A_STEP, CHUNK, P], F32, name="normed_t_f"),
+                        psum.tile([P, BLOCKS_A_STEP, CHUNK, P], F32, name="normed_t_o")]
+            for gate in range(2):
+                for b, j in enumerate(blocks):
+                    for i in range(CHUNK):
+                        nc.tensor.transpose(normed_t[gate][:, b, i, :],
+                                            normed[k][gate][:, i, j * P : (j + 1) * P], ident[:])
+            for gate in range(2):
+                for b, j in enumerate(blocks):
                     nc.scalar.activation(
-                        out=squares[:], in_=y[gate][:], func=ACT.Square,
-                        bias=neg_mean[:, gate : gate + 1], scale=1.0,
-                        accum_out=sum_sq[:, gate : gate + 1],
+                        out=gate_t[k][gate][:, j, :],
+                        in_=normed_t[gate][:, b, :, :].rearrange("p i r -> p (i r)"),
+                        func=ACT.Sigmoid,
+                        scale=affine[:, j, 2 * gate : 2 * gate + 1],
+                        bias=affine[:, j, 2 * gate + 1 : 2 * gate + 2],
                     )
-                var_eps = small.tile([P, 2], F32)
-                nc.gpsimd.tensor_scalar(out=var_eps[:], in0=sum_sq[:], scalar1=1.0 / FEATURES,
-                                        scalar2=EPS, op0=ALU.mult, op1=ALU.add)
-                rstd = small.tile([P, 2], F32)
-                nc.gpsimd.tensor_tensor(out=rstd[:], in0=var_eps[:], in1=neg_half[:], op=ALU.pow)
 
-                gates = [work.tile([P, FEATURES], F32, name="gate_f"),
-                         work.tile([P, FEATURES], F32, name="gate_o")]
-                for gate in range(2):
-                    nc.vector.scalar_tensor_tensor(
-                        out=gates[gate][:], in0=y[gate][:], scalar=neg_mean[:, gate : gate + 1],
-                        in1=gain[:, gate, :], op0=ALU.add, op1=ALU.mult,
-                    )
-                    nc.vector.scalar_tensor_tensor(
-                        out=gates[gate][:], in0=gates[gate][:], scalar=rstd[:, gate : gate + 1],
-                        in1=shift[:, gate, :], op0=ALU.mult, op1=ALU.add,
-                    )
-                    nc.scalar.activation(out=gates[gate][:], in_=gates[gate][:], func=ACT.Sigmoid)
+        def turn_back(t, gate):
+            k, i = divmod(t, CHUNK)
+            back[t, gate] = psum.tile([P, FEATURES], F32, name=("back_f", "back_o")[gate])
+            for j in range(BLOCKS):
+                nc.tensor.transpose(back[t, gate][:, j * P : (j + 1) * P],
+                                    gate_t[k][gate][:, j, i * P : (i + 1) * P], ident[:])
 
-                kept = work.tile([P, FEATURES], F32)
-                nc.vector.tensor_tensor(out=kept[:], in0=gates[FORGET][:], in1=c_sb[:, i, :], op=ALU.mult)
-                nc.vector.tensor_tensor(out=c_new[:, i, :], in0=kept[:], in1=ic_sb[:, i, :], op=ALU.add)
-                squashed = work.tile([P, FEATURES], F32)
-                nc.scalar.activation(out=squashed[:], in_=c_new[:, i, :], func=ACT.Tanh)
-                nc.vector.tensor_tensor(out=h_new[:, i, :], in0=gates[OUTPUT][:], in1=squashed[:], op=ALU.mult)
+        def keep(t):
+            k, i = divmod(t, CHUNK)
+            if i == 0:
+                c_new[k] = stores.tile([P, CHUNK, FEATURES], F32, name="c_new")
+            kept[t] = work.tile([P, FEATURES], F32, name="kept")
+            nc.vector.tensor_tensor(out=kept[t][:], in0=back[t, FORGET][:], in1=c_sb[k][:, i, :], op=ALU.mult)
+            nc.gpsimd.tensor_tensor(out=c_new[k][:, i, :], in0=kept[t][:], in1=ic_sb[k][:, i, :], op=ALU.add)
 
-            nc.sync.dma_start(out=c_new_rows[:, tiles, :], in_=c_new[:])
-            nc.sync.dma_start(out=h_new_rows[:, tiles, :], in_=h_new[:])
+        def squash(t):
+            k, i = divmod(t, CHUNK)
+            squashed[t] = work.tile([P, FEATURES], F32, name="squashed")
+            nc.scalar.activation(out=squashed[t][:], in_=c_new[k][:, i, :], func=ACT.Tanh)
+
+        def put_out(t):
+            k, i = divmod(t, CHUNK)
+            if i == 0:
+                h_new[k] = stores.tile([P, CHUNK, FEATURES], F32, name="h_new")
+            nc.vector.tensor_tensor(out=h_new[k][:, i, :], in0=back[t, OUTPUT][:], in1=squashed[t][:], op=ALU.mult)
+
+        def due(step, lag):
+            return 0 <= step - lag < ROW_TILES
+
+        for step in range(ROW_TILES + LAG_OUT + 1):
+            if step % CHUNK == 0 and step // CHUNK + 1 < CHUNKS:
+                load_x_h(step // CHUNK + 1)
+            if (step - (LAG_KEEP - CHUNK)) % CHUNK == 0 and 0 <= (step - (LAG_KEEP - CHUNK)) // CHUNK < CHUNKS:
+                load_c_ic((step - (LAG_KEEP - CHUNK)) // CHUNK)
+
+            if due(step, LAG_NORMALISE):
+                normalise(step - LAG_NORMALISE)
+            if due(step, LAG_KEEP):
+                keep(step - LAG_KEEP)
+            if due(step, LAG_OUT):
+                put_out(step - LAG_OUT)
+            if due(step, LAG_TANH):
+                squash(step - LAG_TANH)
+            if due(step, LAG_QUANTISE):
+                quantise(step - LAG_QUANTISE)
+            if due(step, LAG_BIAS):
+                add_bias(step - LAG_BIAS)
+            if due(step, 0):
+                turn(step)
+            if due(step, LAG_SQUARES):
+                squares(step - LAG_SQUARES)
+            if due(step, LAG_GATE):
+                gates(step - LAG_GATE)
+            if due(step, LAG_BACK_F):
+                turn_back(step - LAG_BACK_F, FORGET)
+            if due(step, LAG_BACK_O):
+                turn_back(step - LAG_BACK_O, OUTPUT)
+            if due(step, LAG_PRODUCT):
+                products(step - LAG_PRODUCT)
+
+            if due(step, LAG_KEEP) and (step - LAG_KEEP) % CHUNK == CHUNK - 1:
+                k = (step - LAG_KEEP) // CHUNK
+                nc.sync.dma_start(out=c_new_rows[:, chunk_tiles(k), :], in_=c_new[k][:])
+            if due(step, LAG_OUT) and (step - LAG_OUT) % CHUNK == CHUNK - 1:
+                k = (step - LAG_OUT) // CHUNK
+                nc.sync.dma_start(out=h_new_rows[:, chunk_tiles(k), :], in_=h_new[k][:])

@@ -26,6 +26,7 @@ FLOPS = 4 * 2 * ROWS * FEATURES * FEATURES
 
 FORGET, OUTPUT = 0, 1
 
+LAG_REGROUP = 1
 LAG_QUANTISE = 1
 LAG_PRODUCT = 2
 LAG_BIAS = 3
@@ -64,8 +65,8 @@ def tile_layernormlstmcell_pb_t_kernel(
         ctx.enter_context(tc.manual_schedule())
 
         x_sb, h_sb, c_sb, ic_sb, c_new, h_new = {}, {}, {}, {}, {}, {}
-        grouped, xh_codes, xh_scales, pre, y = {}, {}, {}, {}, {}
-        neg_mean, rstd, normed, gate_t, back, kept, squashed = {}, {}, {}, {}, {}, {}, {}
+        turned, grouped, xh_codes, xh_scales, pre, y = {}, {}, {}, {}, {}, {}
+        neg_mean, sum_sq, rstd, normed, normed_t, gate_t, back, kept, squashed = {}, {}, {}, {}, {}, {}, {}, {}, {}
 
         def chunk_tiles(k):
             return slice(k * CHUNK, (k + 1) * CHUNK)
@@ -126,17 +127,15 @@ def tile_layernormlstmcell_pb_t_kernel(
 
         def turn(t):
             k, i = divmod(t, CHUNK)
-            turned = psum.tile([P, 2, 2, P], F32, name="turned")
+            turned[t] = psum.tile([P, 2, 2, P], F32, name="turned")
             for a, source in enumerate((x_sb[k], h_sb[k])):
                 pairs = source[:, i, :].bitcast(F32)
                 for u in range(2):
-                    nc.tensor.transpose(turned[:, a, u, :], pairs[:, u:WORDS:2], ident[:])
+                    nc.tensor.transpose(turned[t][:, a, u, :], pairs[:, u:WORDS:2], ident[:])
+
+        def regroup(t):
             grouped[t] = work.tile([P, 2, P, 4], BF16, name="grouped", align_bytes=64)
-            side_by_side = turned[:].rearrange("p a u r -> p a r u")
-            if t % 2 == 0:
-                nc.scalar.copy(out=grouped[t][:].bitcast(F32), in_=side_by_side)
-            else:
-                nc.vector.tensor_copy(out=grouped[t][:].bitcast(F32), in_=side_by_side)
+            nc.scalar.copy(out=grouped[t][:].bitcast(F32), in_=turned[t][:].rearrange("p a u r -> p a r u"))
 
         def quantise(t):
             xh_codes[t] = work.tile([P, 2 * P], U32, name="xh_codes", align_bytes=64)
@@ -147,21 +146,21 @@ def tile_layernormlstmcell_pb_t_kernel(
                 in_=grouped[t][:].rearrange("p a r t -> p (a r t)"),
             )
 
-        def products(t):
-            pre[t] = [psum.tile([P, FEATURES], F32, name="pre_f", tag="pre", bufs=3),
-                      psum.tile([P, FEATURES], F32, name="pre_o", tag="pre", bufs=3)]
-            for a in range(2):
-                for gate in range(2):
-                    w = 2 * gate + a
-                    nc.tensor.matmul_mx(
-                        out=pre[t][gate][:],
-                        lhsT=xh_codes[t][:, a * P : (a + 1) * P].bitcast(FP8X4),
-                        lhsT_scale=xh_scales[t][:, a * P : (a + 1) * P],
-                        rhs=w_codes[:, w, :].bitcast(FP8X4),
-                        rhs_scale=w_scales[:, w, :],
-                        start=(a == 0),
-                        stop=(a == 1),
-                    )
+        def products(t, a):
+            if a == 0:
+                pre[t] = [psum.tile([P, FEATURES], F32, name="pre_f", tag="pre", bufs=3),
+                          psum.tile([P, FEATURES], F32, name="pre_o", tag="pre", bufs=3)]
+            for gate in range(2):
+                w = 2 * gate + a
+                nc.tensor.matmul_mx(
+                    out=pre[t][gate][:],
+                    lhsT=xh_codes[t][:, a * P : (a + 1) * P].bitcast(FP8X4),
+                    lhsT_scale=xh_scales[t][:, a * P : (a + 1) * P],
+                    rhs=w_codes[:, w, :].bitcast(FP8X4),
+                    rhs_scale=w_scales[:, w, :],
+                    start=(a == 0),
+                    stop=(a == 1),
+                )
 
         def add_bias(t):
             y[t] = [work.tile([P, FEATURES], F32, name="y_f", bufs=4),
@@ -176,16 +175,18 @@ def tile_layernormlstmcell_pb_t_kernel(
             nc.vector.tensor_scalar_mul(out=neg_mean[t][:], in0=row_sum[:], scalar1=-1.0 / FEATURES)
 
         def squares(t):
-            sum_sq = small.tile([P, 2], F32, name="sum_sq")
+            sum_sq[t] = small.tile([P, 2], F32, name="sum_sq")
             for gate in range(2):
                 unused = work.tile([P, FEATURES], BF16, name="unused")
                 nc.scalar.activation(
                     out=unused[:], in_=y[t][gate][:], func=ACT.Square,
                     bias=neg_mean[t][:, gate : gate + 1], scale=1.0,
-                    accum_out=sum_sq[:, gate : gate + 1],
+                    accum_out=sum_sq[t][:, gate : gate + 1],
                 )
+
+        def inverse_deviation(t):
             var_eps = small.tile([P, 2], F32, name="var_eps")
-            nc.gpsimd.tensor_scalar(out=var_eps[:], in0=sum_sq[:], scalar1=1.0 / FEATURES,
+            nc.gpsimd.tensor_scalar(out=var_eps[:], in0=sum_sq[t][:], scalar1=1.0 / FEATURES,
                                     scalar2=EPS, op0=ALU.mult, op1=ALU.add)
             rstd[t] = small.tile([P, 2], F32, name="rstd")
             nc.gpsimd.tensor_tensor(out=rstd[t][:], in0=var_eps[:], in1=neg_half[:], op=ALU.pow)
@@ -195,35 +196,37 @@ def tile_layernormlstmcell_pb_t_kernel(
             if i == 0:
                 normed[k] = [chunks.tile([P, CHUNK, FEATURES], F32, name="normed_f"),
                              chunks.tile([P, CHUNK, FEATURES], F32, name="normed_o")]
-            nc.gpsimd.tensor_scalar(
-                out=normed[k][FORGET][:, i, :], in0=y[t][FORGET][:],
-                scalar1=neg_mean[t][:, FORGET : FORGET + 1], scalar2=rstd[t][:, FORGET : FORGET + 1],
-                op0=ALU.add, op1=ALU.mult,
-            )
-            nc.vector.tensor_scalar(
-                out=normed[k][OUTPUT][:, i, :], in0=y[t][OUTPUT][:],
-                scalar1=neg_mean[t][:, OUTPUT : OUTPUT + 1], scalar2=rstd[t][:, OUTPUT : OUTPUT + 1],
-                op0=ALU.add, op1=ALU.mult,
-            )
+            for gate in range(2):
+                nc.vector.tensor_scalar(
+                    out=normed[k][gate][:, i, :], in0=y[t][gate][:],
+                    scalar1=neg_mean[t][:, gate : gate + 1], scalar2=rstd[t][:, gate : gate + 1],
+                    op0=ALU.add, op1=ALU.mult,
+                )
 
-        def gates(unit):
+        def blocks_of(unit):
             k, part = divmod(unit, CHUNK)
-            if part == 0:
-                gate_t[k] = [chunks.tile([P, BLOCKS, CHUNK * P], F32, name="gate_t_f"),
-                             chunks.tile([P, BLOCKS, CHUNK * P], F32, name="gate_t_o", bufs=3)]
-            blocks = range(part * BLOCKS_A_STEP, (part + 1) * BLOCKS_A_STEP)
-            normed_t = [psum.tile([P, BLOCKS_A_STEP, CHUNK, P], F32, name="normed_t_f"),
-                        psum.tile([P, BLOCKS_A_STEP, CHUNK, P], F32, name="normed_t_o")]
+            return k, range(part * BLOCKS_A_STEP, (part + 1) * BLOCKS_A_STEP)
+
+        def turn_normed(unit):
+            k, blocks = blocks_of(unit)
+            normed_t[unit] = [psum.tile([P, BLOCKS_A_STEP, CHUNK, P], F32, name="normed_t_f"),
+                              psum.tile([P, BLOCKS_A_STEP, CHUNK, P], F32, name="normed_t_o")]
             for gate in range(2):
                 for b, j in enumerate(blocks):
                     for i in range(CHUNK):
-                        nc.tensor.transpose(normed_t[gate][:, b, i, :],
+                        nc.tensor.transpose(normed_t[unit][gate][:, b, i, :],
                                             normed[k][gate][:, i, j * P : (j + 1) * P], ident[:])
+
+        def sigmoids(unit):
+            k, blocks = blocks_of(unit)
+            if unit % CHUNK == 0:
+                gate_t[k] = [chunks.tile([P, BLOCKS, CHUNK * P], F32, name="gate_t_f"),
+                             chunks.tile([P, BLOCKS, CHUNK * P], F32, name="gate_t_o", bufs=3)]
             for gate in range(2):
                 for b, j in enumerate(blocks):
                     nc.scalar.activation(
                         out=gate_t[k][gate][:, j, :],
-                        in_=normed_t[gate][:, b, :, :].rearrange("p i r -> p (i r)"),
+                        in_=normed_t[unit][gate][:, b, :, :].rearrange("p i r -> p (i r)"),
                         func=ACT.Sigmoid,
                         scale=affine[:, j, 2 * gate : 2 * gate + 1],
                         bias=affine[:, j, 2 * gate + 1 : 2 * gate + 2],
@@ -238,10 +241,13 @@ def tile_layernormlstmcell_pb_t_kernel(
 
         def keep(t):
             k, i = divmod(t, CHUNK)
-            if i == 0:
-                c_new[k] = stores.tile([P, CHUNK, FEATURES], F32, name="c_new")
             kept[t] = work.tile([P, FEATURES], F32, name="kept")
             nc.vector.tensor_tensor(out=kept[t][:], in0=back[t, FORGET][:], in1=c_sb[k][:, i, :], op=ALU.mult)
+
+        def add_input(t):
+            k, i = divmod(t, CHUNK)
+            if i == 0:
+                c_new[k] = stores.tile([P, CHUNK, FEATURES], F32, name="c_new")
             nc.gpsimd.tensor_tensor(out=c_new[k][:, i, :], in0=kept[t][:], in1=ic_sb[k][:, i, :], op=ALU.add)
 
         def squash(t):
@@ -264,30 +270,40 @@ def tile_layernormlstmcell_pb_t_kernel(
             if (step - (LAG_KEEP - CHUNK)) % CHUNK == 0 and 0 <= (step - (LAG_KEEP - CHUNK)) // CHUNK < CHUNKS:
                 load_c_ic((step - (LAG_KEEP - CHUNK)) // CHUNK)
 
-            if due(step, LAG_NORMALISE):
-                normalise(step - LAG_NORMALISE)
             if due(step, LAG_KEEP):
                 keep(step - LAG_KEEP)
-            if due(step, LAG_OUT):
-                put_out(step - LAG_OUT)
-            if due(step, LAG_TANH):
-                squash(step - LAG_TANH)
-            if due(step, LAG_QUANTISE):
-                quantise(step - LAG_QUANTISE)
+            if due(step, LAG_NORMALISE):
+                inverse_deviation(step - LAG_NORMALISE)
+            if due(step, LAG_KEEP):
+                add_input(step - LAG_KEEP)
             if due(step, LAG_BIAS):
                 add_bias(step - LAG_BIAS)
-            if due(step, 0):
-                turn(step)
-            if due(step, LAG_SQUARES):
-                squares(step - LAG_SQUARES)
-            if due(step, LAG_GATE):
-                gates(step - LAG_GATE)
+            if due(step, LAG_PRODUCT):
+                products(step - LAG_PRODUCT, 0)
+            if due(step, LAG_OUT):
+                put_out(step - LAG_OUT)
             if due(step, LAG_BACK_F):
                 turn_back(step - LAG_BACK_F, FORGET)
+            if due(step, LAG_GATE):
+                turn_normed(step - LAG_GATE)
+            if due(step, LAG_TANH):
+                squash(step - LAG_TANH)
+            if due(step, LAG_REGROUP):
+                regroup(step - LAG_REGROUP)
+            if due(step, LAG_SQUARES):
+                squares(step - LAG_SQUARES)
+            if due(step, LAG_NORMALISE):
+                normalise(step - LAG_NORMALISE)
+            if due(step, LAG_PRODUCT):
+                products(step - LAG_PRODUCT, 1)
+            if due(step, LAG_GATE):
+                sigmoids(step - LAG_GATE)
+            if due(step, LAG_QUANTISE):
+                quantise(step - LAG_QUANTISE)
             if due(step, LAG_BACK_O):
                 turn_back(step - LAG_BACK_O, OUTPUT)
-            if due(step, LAG_PRODUCT):
-                products(step - LAG_PRODUCT)
+            if due(step, 0):
+                turn(step)
 
             if due(step, LAG_KEEP) and (step - LAG_KEEP) % CHUNK == CHUNK - 1:
                 k = (step - LAG_KEEP) // CHUNK

@@ -17,9 +17,10 @@ ROWS = 4096
 FEATURES = 512
 ROW_TILES = ROWS // P
 BLOCKS = FEATURES // P
-CHUNK = 4
+CHUNK = 2
 CHUNKS = ROW_TILES // CHUNK
 BLOCKS_A_STEP = BLOCKS // CHUNK
+LOAD_AHEAD = 2
 WORDS = FEATURES // 2
 EPS = 1e-5
 FLOPS = 4 * 2 * ROWS * FEATURES * FEATURES
@@ -56,8 +57,8 @@ def tile_layernormlstmcell_pb_t_kernel(
 
     with ExitStack() as ctx:
         const = ctx.enter_context(tc.tile_pool(name="const", bufs=1))
-        loads = ctx.enter_context(tc.tile_pool(name="loads", bufs=2))
-        stores = ctx.enter_context(tc.tile_pool(name="stores", bufs=2))
+        loads = ctx.enter_context(tc.tile_pool(name="loads", bufs=LOAD_AHEAD + 1))
+        stores = ctx.enter_context(tc.tile_pool(name="stores", bufs=3))
         work = ctx.enter_context(tc.tile_pool(name="work", bufs=3))
         chunks = ctx.enter_context(tc.tile_pool(name="chunks", bufs=2))
         small = ctx.enter_context(tc.tile_pool(name="small", bufs=4))
@@ -101,6 +102,8 @@ def tile_layernormlstmcell_pb_t_kernel(
                 out=w_codes[:, w, :].bitcast(I32),
                 in_=code_bytes.rearrange("g p n t -> (g p) (n t)").bitcast(I32),
             )
+
+        load_x_h(1)
 
         ident = const.tile([P, P], F32)
         make_identity(nc, ident[:])
@@ -265,10 +268,12 @@ def tile_layernormlstmcell_pb_t_kernel(
             return 0 <= step - lag < ROW_TILES
 
         for step in range(ROW_TILES + LAG_OUT + 1):
-            if step % CHUNK == 0 and step // CHUNK + 1 < CHUNKS:
-                load_x_h(step // CHUNK + 1)
-            if (step - (LAG_KEEP - CHUNK)) % CHUNK == 0 and 0 <= (step - (LAG_KEEP - CHUNK)) // CHUNK < CHUNKS:
-                load_c_ic((step - (LAG_KEEP - CHUNK)) // CHUNK)
+            if step % CHUNK == 0:
+                if step // CHUNK + LOAD_AHEAD < CHUNKS:
+                    load_x_h(step // CHUNK + LOAD_AHEAD)
+            if (step - LAG_KEEP) % CHUNK == 0:
+                if 0 <= (step - LAG_KEEP) // CHUNK + LOAD_AHEAD < CHUNKS:
+                    load_c_ic((step - LAG_KEEP) // CHUNK + LOAD_AHEAD)
 
             if due(step, LAG_KEEP):
                 keep(step - LAG_KEEP)

@@ -149,21 +149,21 @@ def tile_layernormlstmcell_pb_t_kernel(
                 in_=grouped[t][:].rearrange("p a r t -> p (a r t)"),
             )
 
-        def products(t, a):
-            if a == 0:
-                pre[t] = [psum.tile([P, FEATURES], F32, name="pre_f", tag="pre", bufs=3),
-                          psum.tile([P, FEATURES], F32, name="pre_o", tag="pre", bufs=3)]
+        def products(t):
+            pre[t] = [psum.tile([P, FEATURES], F32, name="pre_f", tag="pre", bufs=3),
+                      psum.tile([P, FEATURES], F32, name="pre_o", tag="pre", bufs=3)]
             for gate in range(2):
-                w = 2 * gate + a
-                nc.tensor.matmul_mx(
-                    out=pre[t][gate][:],
-                    lhsT=xh_codes[t][:, a * P : (a + 1) * P].bitcast(FP8X4),
-                    lhsT_scale=xh_scales[t][:, a * P : (a + 1) * P],
-                    rhs=w_codes[:, w, :].bitcast(FP8X4),
-                    rhs_scale=w_scales[:, w, :],
-                    start=(a == 0),
-                    stop=(a == 1),
-                )
+                for a in range(2):
+                    w = 2 * gate + a
+                    nc.tensor.matmul_mx(
+                        out=pre[t][gate][:],
+                        lhsT=xh_codes[t][:, a * P : (a + 1) * P].bitcast(FP8X4),
+                        lhsT_scale=xh_scales[t][:, a * P : (a + 1) * P],
+                        rhs=w_codes[:, w, :].bitcast(FP8X4),
+                        rhs_scale=w_scales[:, w, :],
+                        start=(a == 0),
+                        stop=(a == 1),
+                    )
 
         def add_bias(t):
             y[t] = [work.tile([P, FEATURES], F32, name="y_f", bufs=4),
@@ -284,7 +284,7 @@ def tile_layernormlstmcell_pb_t_kernel(
             if due(step, LAG_BIAS):
                 add_bias(step - LAG_BIAS)
             if due(step, LAG_PRODUCT):
-                products(step - LAG_PRODUCT, 0)
+                products(step - LAG_PRODUCT)
             if due(step, LAG_OUT):
                 put_out(step - LAG_OUT)
             if due(step, LAG_BACK_F):
@@ -299,8 +299,6 @@ def tile_layernormlstmcell_pb_t_kernel(
                 squares(step - LAG_SQUARES)
             if due(step, LAG_NORMALISE):
                 normalise(step - LAG_NORMALISE)
-            if due(step, LAG_PRODUCT):
-                products(step - LAG_PRODUCT, 1)
             if due(step, LAG_GATE):
                 sigmoids(step - LAG_GATE)
             if due(step, LAG_QUANTISE):

@@ -17,9 +17,8 @@ ROWS = 4096
 FEATURES = 512
 ROW_TILES = ROWS // P
 BLOCKS = FEATURES // P
-CHUNK = 2
-CHUNKS = ROW_TILES // CHUNK
-BLOCKS_A_STEP = BLOCKS // CHUNK
+PAIR = 2
+PAIRS = ROW_TILES // PAIR
 LOAD_AHEAD = 2
 WORDS = FEATURES // 2
 EPS = 1e-5
@@ -33,12 +32,12 @@ LAG_PRODUCT = 2
 LAG_BIAS = 3
 LAG_SQUARES = 4
 LAG_NORMALISE = 5
-LAG_GATE = LAG_NORMALISE + CHUNK
-LAG_BACK_F = LAG_GATE + CHUNK
+LAG_GATE = LAG_NORMALISE + PAIR
+LAG_BACK_F = LAG_GATE + 1
 LAG_KEEP = LAG_BACK_F + 1
+LAG_BACK_O = LAG_GATE + PAIR
 LAG_TANH = LAG_KEEP + 1
-LAG_BACK_O = LAG_TANH
-LAG_OUT = LAG_BACK_O + 1
+LAG_OUT = LAG_TANH
 
 
 def tile_layernormlstmcell_pb_t_kernel(
@@ -60,29 +59,30 @@ def tile_layernormlstmcell_pb_t_kernel(
         loads = ctx.enter_context(tc.tile_pool(name="loads", bufs=LOAD_AHEAD + 1))
         stores = ctx.enter_context(tc.tile_pool(name="stores", bufs=3))
         work = ctx.enter_context(tc.tile_pool(name="work", bufs=3))
-        chunks = ctx.enter_context(tc.tile_pool(name="chunks", bufs=2))
+        pairs = ctx.enter_context(tc.tile_pool(name="pairs", bufs=2))
         small = ctx.enter_context(tc.tile_pool(name="small", bufs=4))
         psum = ctx.enter_context(tc.psum_pool(name="psum", bufs=1))
         ctx.enter_context(tc.manual_schedule())
 
         x_sb, h_sb, c_sb, ic_sb, c_new, h_new = {}, {}, {}, {}, {}, {}
         turned, grouped, xh_codes, xh_scales, pre, y = {}, {}, {}, {}, {}, {}
-        neg_mean, sum_sq, rstd, normed, normed_t, gate_t, back, kept, squashed = {}, {}, {}, {}, {}, {}, {}, {}, {}
+        row_sum, neg_mean, sum_sq, var_eps, rstd = {}, {}, {}, {}, {}
+        normed, normed_t, gate_t, back, kept, squashed = {}, {}, {}, {}, {}, {}
 
-        def chunk_tiles(k):
-            return slice(k * CHUNK, (k + 1) * CHUNK)
+        def tiles_of(k):
+            return slice(k * PAIR, (k + 1) * PAIR)
 
         def load_x_h(k):
-            x_sb[k] = loads.tile([P, CHUNK, FEATURES], BF16, name="x_sb")
-            h_sb[k] = loads.tile([P, CHUNK, FEATURES], BF16, name="h_sb")
-            nc.sync.dma_start(out=x_sb[k][:], in_=x_rows[:, chunk_tiles(k), :])
-            nc.sync.dma_start(out=h_sb[k][:], in_=h_rows[:, chunk_tiles(k), :])
+            x_sb[k] = loads.tile([P, PAIR, FEATURES], BF16, name="x_sb")
+            h_sb[k] = loads.tile([P, PAIR, FEATURES], BF16, name="h_sb")
+            nc.sync.dma_start(out=x_sb[k][:], in_=x_rows[:, tiles_of(k), :])
+            nc.sync.dma_start(out=h_sb[k][:], in_=h_rows[:, tiles_of(k), :])
 
         def load_c_ic(k):
-            c_sb[k] = loads.tile([P, CHUNK, FEATURES], BF16, name="c_sb")
-            ic_sb[k] = loads.tile([P, CHUNK, FEATURES], BF16, name="ic_sb")
-            nc.sync.dma_start(out=c_sb[k][:], in_=c_rows[:, chunk_tiles(k), :])
-            nc.sync.dma_start(out=ic_sb[k][:], in_=ic_rows[:, chunk_tiles(k), :])
+            c_sb[k] = loads.tile([P, PAIR, FEATURES], BF16, name="c_sb")
+            ic_sb[k] = loads.tile([P, PAIR, FEATURES], BF16, name="ic_sb")
+            nc.sync.dma_start(out=c_sb[k][:], in_=c_rows[:, tiles_of(k), :])
+            nc.sync.dma_start(out=ic_sb[k][:], in_=ic_rows[:, tiles_of(k), :])
 
         load_x_h(0)
 
@@ -102,7 +102,6 @@ def tile_layernormlstmcell_pb_t_kernel(
                 out=w_codes[:, w, :].bitcast(I32),
                 in_=code_bytes.rearrange("g p n t -> (g p) (n t)").bitcast(I32),
             )
-
         load_x_h(1)
 
         ident = const.tile([P, P], F32)
@@ -129,12 +128,12 @@ def tile_layernormlstmcell_pb_t_kernel(
             nc.vector.tensor_copy(out=bias[:, gate, :], in_=spread[:])
 
         def turn(t):
-            k, i = divmod(t, CHUNK)
+            k, i = divmod(t, PAIR)
             turned[t] = psum.tile([P, 2, 2, P], F32, name="turned")
             for a, source in enumerate((x_sb[k], h_sb[k])):
-                pairs = source[:, i, :].bitcast(F32)
+                words = source[:, i, :].bitcast(F32)
                 for u in range(2):
-                    nc.tensor.transpose(turned[t][:, a, u, :], pairs[:, u:WORDS:2], ident[:])
+                    nc.tensor.transpose(turned[t][:, a, u, :], words[:, u:WORDS:2], ident[:])
 
         def regroup(t):
             grouped[t] = work.tile([P, 2, P, 4], BF16, name="grouped", align_bytes=64)
@@ -149,33 +148,35 @@ def tile_layernormlstmcell_pb_t_kernel(
                 in_=grouped[t][:].rearrange("p a r t -> p (a r t)"),
             )
 
-        def products(t):
-            pre[t] = [psum.tile([P, FEATURES], F32, name="pre_f", tag="pre", bufs=3),
-                      psum.tile([P, FEATURES], F32, name="pre_o", tag="pre", bufs=3)]
+        def products(t, a):
+            if a == 0:
+                pre[t] = [psum.tile([P, FEATURES], F32, name="pre_f", tag="pre", bufs=3),
+                          psum.tile([P, FEATURES], F32, name="pre_o", tag="pre", bufs=3)]
             for gate in range(2):
-                for a in range(2):
-                    w = 2 * gate + a
-                    nc.tensor.matmul_mx(
-                        out=pre[t][gate][:],
-                        lhsT=xh_codes[t][:, a * P : (a + 1) * P].bitcast(FP8X4),
-                        lhsT_scale=xh_scales[t][:, a * P : (a + 1) * P],
-                        rhs=w_codes[:, w, :].bitcast(FP8X4),
-                        rhs_scale=w_scales[:, w, :],
-                        start=(a == 0),
-                        stop=(a == 1),
-                    )
+                w = 2 * gate + a
+                nc.tensor.matmul_mx(
+                    out=pre[t][gate][:],
+                    lhsT=xh_codes[t][:, a * P : (a + 1) * P].bitcast(FP8X4),
+                    lhsT_scale=xh_scales[t][:, a * P : (a + 1) * P],
+                    rhs=w_codes[:, w, :].bitcast(FP8X4),
+                    rhs_scale=w_scales[:, w, :],
+                    start=(a == 0),
+                    stop=(a == 1),
+                )
 
         def add_bias(t):
             y[t] = [work.tile([P, FEATURES], F32, name="y_f", bufs=4),
                     work.tile([P, FEATURES], F32, name="y_o", bufs=4)]
-            row_sum = small.tile([P, 2], F32, name="row_sum")
+            row_sum[t] = small.tile([P, 2], F32, name="row_sum")
             for gate in range(2):
                 nc.vector.scalar_tensor_tensor(
                     out=y[t][gate][:], in0=pre[t][gate][:], scalar=1.0, in1=bias[:, gate, :],
-                    op0=ALU.mult, op1=ALU.add, accum_out=row_sum[:, gate : gate + 1],
+                    op0=ALU.mult, op1=ALU.add, accum_out=row_sum[t][:, gate : gate + 1],
                 )
+
+        def mean(t):
             neg_mean[t] = small.tile([P, 2], F32, name="neg_mean")
-            nc.vector.tensor_scalar_mul(out=neg_mean[t][:], in0=row_sum[:], scalar1=-1.0 / FEATURES)
+            nc.vector.tensor_scalar_mul(out=neg_mean[t][:], in0=row_sum[t][:], scalar1=-1.0 / FEATURES)
 
         def squares(t):
             sum_sq[t] = small.tile([P, 2], F32, name="sum_sq")
@@ -187,18 +188,20 @@ def tile_layernormlstmcell_pb_t_kernel(
                     accum_out=sum_sq[t][:, gate : gate + 1],
                 )
 
-        def inverse_deviation(t):
-            var_eps = small.tile([P, 2], F32, name="var_eps")
-            nc.gpsimd.tensor_scalar(out=var_eps[:], in0=sum_sq[t][:], scalar1=1.0 / FEATURES,
+        def variance(t):
+            var_eps[t] = small.tile([P, 2], F32, name="var_eps")
+            nc.vector.tensor_scalar(out=var_eps[t][:], in0=sum_sq[t][:], scalar1=1.0 / FEATURES,
                                     scalar2=EPS, op0=ALU.mult, op1=ALU.add)
+
+        def inverse_deviation(t):
             rstd[t] = small.tile([P, 2], F32, name="rstd")
-            nc.gpsimd.tensor_tensor(out=rstd[t][:], in0=var_eps[:], in1=neg_half[:], op=ALU.pow)
+            nc.gpsimd.tensor_tensor(out=rstd[t][:], in0=var_eps[t][:], in1=neg_half[:], op=ALU.pow)
 
         def normalise(t):
-            k, i = divmod(t, CHUNK)
+            k, i = divmod(t, PAIR)
             if i == 0:
-                normed[k] = [chunks.tile([P, CHUNK, FEATURES], F32, name="normed_f"),
-                             chunks.tile([P, CHUNK, FEATURES], F32, name="normed_o")]
+                normed[k] = [pairs.tile([P, PAIR, FEATURES], F32, name="normed_f"),
+                             pairs.tile([P, PAIR, FEATURES], F32, name="normed_o")]
             for gate in range(2):
                 nc.vector.tensor_scalar(
                     out=normed[k][gate][:, i, :], in0=y[t][gate][:],
@@ -206,74 +209,64 @@ def tile_layernormlstmcell_pb_t_kernel(
                     op0=ALU.add, op1=ALU.mult,
                 )
 
-        def blocks_of(unit):
-            k, part = divmod(unit, CHUNK)
-            return k, range(part * BLOCKS_A_STEP, (part + 1) * BLOCKS_A_STEP)
+        def turn_normed(k, gate):
+            normed_t[k, gate] = [psum.tile([P, 2, PAIR, P], F32, name="normed_t_low"),
+                                 psum.tile([P, 2, PAIR, P], F32, name="normed_t_high")]
+            for j in range(BLOCKS):
+                for i in range(PAIR):
+                    nc.tensor.transpose(normed_t[k, gate][j // 2][:, j % 2, i, :],
+                                        normed[k][gate][:, i, j * P : (j + 1) * P], ident[:])
 
-        def turn_normed(unit):
-            k, blocks = blocks_of(unit)
-            normed_t[unit] = [psum.tile([P, BLOCKS_A_STEP, CHUNK, P], F32, name="normed_t_f"),
-                              psum.tile([P, BLOCKS_A_STEP, CHUNK, P], F32, name="normed_t_o")]
-            for gate in range(2):
-                for b, j in enumerate(blocks):
-                    for i in range(CHUNK):
-                        nc.tensor.transpose(normed_t[unit][gate][:, b, i, :],
-                                            normed[k][gate][:, i, j * P : (j + 1) * P], ident[:])
-
-        def sigmoids(unit):
-            k, blocks = blocks_of(unit)
-            if unit % CHUNK == 0:
-                gate_t[k] = [chunks.tile([P, BLOCKS, CHUNK * P], F32, name="gate_t_f"),
-                             chunks.tile([P, BLOCKS, CHUNK * P], F32, name="gate_t_o", bufs=3)]
-            for gate in range(2):
-                for b, j in enumerate(blocks):
-                    nc.scalar.activation(
-                        out=gate_t[k][gate][:, j, :],
-                        in_=normed_t[unit][gate][:, b, :, :].rearrange("p i r -> p (i r)"),
-                        func=ACT.Sigmoid,
-                        scale=affine[:, j, 2 * gate : 2 * gate + 1],
-                        bias=affine[:, j, 2 * gate + 1 : 2 * gate + 2],
-                    )
+        def sigmoids(k, gate):
+            gate_t[k, gate] = pairs.tile([P, BLOCKS, PAIR * P], F32, name=("gate_t_f", "gate_t_o")[gate])
+            for j in range(BLOCKS):
+                nc.scalar.activation(
+                    out=gate_t[k, gate][:, j, :],
+                    in_=normed_t[k, gate][j // 2][:, j % 2, :, :].rearrange("p i r -> p (i r)"),
+                    func=ACT.Sigmoid,
+                    scale=affine[:, j, 2 * gate : 2 * gate + 1],
+                    bias=affine[:, j, 2 * gate + 1 : 2 * gate + 2],
+                )
 
         def turn_back(t, gate):
-            k, i = divmod(t, CHUNK)
+            k, i = divmod(t, PAIR)
             back[t, gate] = psum.tile([P, FEATURES], F32, name=("back_f", "back_o")[gate])
             for j in range(BLOCKS):
                 nc.tensor.transpose(back[t, gate][:, j * P : (j + 1) * P],
-                                    gate_t[k][gate][:, j, i * P : (i + 1) * P], ident[:])
+                                    gate_t[k, gate][:, j, i * P : (i + 1) * P], ident[:])
 
         def keep(t):
-            k, i = divmod(t, CHUNK)
+            k, i = divmod(t, PAIR)
             kept[t] = work.tile([P, FEATURES], F32, name="kept")
             nc.vector.tensor_tensor(out=kept[t][:], in0=back[t, FORGET][:], in1=c_sb[k][:, i, :], op=ALU.mult)
 
         def add_input(t):
-            k, i = divmod(t, CHUNK)
+            k, i = divmod(t, PAIR)
             if i == 0:
-                c_new[k] = stores.tile([P, CHUNK, FEATURES], F32, name="c_new")
+                c_new[k] = stores.tile([P, PAIR, FEATURES], F32, name="c_new")
             nc.gpsimd.tensor_tensor(out=c_new[k][:, i, :], in0=kept[t][:], in1=ic_sb[k][:, i, :], op=ALU.add)
 
         def squash(t):
-            k, i = divmod(t, CHUNK)
+            k, i = divmod(t, PAIR)
             squashed[t] = work.tile([P, FEATURES], F32, name="squashed")
             nc.scalar.activation(out=squashed[t][:], in_=c_new[k][:, i, :], func=ACT.Tanh)
 
         def put_out(t):
-            k, i = divmod(t, CHUNK)
+            k, i = divmod(t, PAIR)
             if i == 0:
-                h_new[k] = stores.tile([P, CHUNK, FEATURES], F32, name="h_new")
+                h_new[k] = stores.tile([P, PAIR, FEATURES], F32, name="h_new")
             nc.vector.tensor_tensor(out=h_new[k][:, i, :], in0=back[t, OUTPUT][:], in1=squashed[t][:], op=ALU.mult)
 
         def due(step, lag):
             return 0 <= step - lag < ROW_TILES
 
         for step in range(ROW_TILES + LAG_OUT + 1):
-            if step % CHUNK == 0:
-                if step // CHUNK + LOAD_AHEAD < CHUNKS:
-                    load_x_h(step // CHUNK + LOAD_AHEAD)
-            if (step - LAG_KEEP) % CHUNK == 0:
-                if 0 <= (step - LAG_KEEP) // CHUNK + LOAD_AHEAD < CHUNKS:
-                    load_c_ic((step - LAG_KEEP) // CHUNK + LOAD_AHEAD)
+            if step % PAIR == 0:
+                if step // PAIR + LOAD_AHEAD < PAIRS:
+                    load_x_h(step // PAIR + LOAD_AHEAD)
+            if (step - LAG_KEEP) % PAIR == 0:
+                if 0 <= (step - LAG_KEEP) // PAIR + LOAD_AHEAD < PAIRS:
+                    load_c_ic((step - LAG_KEEP) // PAIR + LOAD_AHEAD)
 
             if due(step, LAG_KEEP):
                 keep(step - LAG_KEEP)
@@ -281,36 +274,42 @@ def tile_layernormlstmcell_pb_t_kernel(
                 inverse_deviation(step - LAG_NORMALISE)
             if due(step, LAG_KEEP):
                 add_input(step - LAG_KEEP)
+            if due(step, LAG_TANH):
+                squash(step - LAG_TANH)
             if due(step, LAG_BIAS):
                 add_bias(step - LAG_BIAS)
             if due(step, LAG_PRODUCT):
-                products(step - LAG_PRODUCT)
+                products(step - LAG_PRODUCT, 0)
             if due(step, LAG_OUT):
                 put_out(step - LAG_OUT)
             if due(step, LAG_BACK_F):
                 turn_back(step - LAG_BACK_F, FORGET)
             if due(step, LAG_GATE):
-                turn_normed(step - LAG_GATE)
-            if due(step, LAG_TANH):
-                squash(step - LAG_TANH)
+                turn_normed((step - LAG_GATE) // PAIR, (step - LAG_GATE) % PAIR)
             if due(step, LAG_REGROUP):
                 regroup(step - LAG_REGROUP)
             if due(step, LAG_SQUARES):
                 squares(step - LAG_SQUARES)
+            if due(step, LAG_BIAS):
+                mean(step - LAG_BIAS)
             if due(step, LAG_NORMALISE):
                 normalise(step - LAG_NORMALISE)
+            if due(step, LAG_PRODUCT):
+                products(step - LAG_PRODUCT, 1)
             if due(step, LAG_GATE):
-                sigmoids(step - LAG_GATE)
+                sigmoids((step - LAG_GATE) // PAIR, (step - LAG_GATE) % PAIR)
             if due(step, LAG_QUANTISE):
                 quantise(step - LAG_QUANTISE)
+            if due(step, LAG_SQUARES):
+                variance(step - LAG_SQUARES)
             if due(step, LAG_BACK_O):
                 turn_back(step - LAG_BACK_O, OUTPUT)
             if due(step, 0):
                 turn(step)
 
-            if due(step, LAG_KEEP) and (step - LAG_KEEP) % CHUNK == CHUNK - 1:
-                k = (step - LAG_KEEP) // CHUNK
-                nc.sync.dma_start(out=c_new_rows[:, chunk_tiles(k), :], in_=c_new[k][:])
-            if due(step, LAG_OUT) and (step - LAG_OUT) % CHUNK == CHUNK - 1:
-                k = (step - LAG_OUT) // CHUNK
-                nc.sync.dma_start(out=h_new_rows[:, chunk_tiles(k), :], in_=h_new[k][:])
+            if due(step, LAG_KEEP) and (step - LAG_KEEP) % PAIR == PAIR - 1:
+                k = (step - LAG_KEEP) // PAIR
+                nc.sync.dma_start(out=c_new_rows[:, tiles_of(k), :], in_=c_new[k][:])
+            if due(step, LAG_OUT) and (step - LAG_OUT) % PAIR == PAIR - 1:
+                k = (step - LAG_OUT) // PAIR
+                nc.sync.dma_start(out=h_new_rows[:, tiles_of(k), :], in_=h_new[k][:])

@@ -26,18 +26,17 @@ FLOPS = 4 * 2 * ROWS * FEATURES * FEATURES
 
 FORGET, OUTPUT = 0, 1
 
-LAG_REGROUP = 1
 LAG_QUANTISE = 1
-LAG_PRODUCT = 2
-LAG_BIAS = 3
-LAG_SQUARES = 4
-LAG_NORMALISE = 5
+AHEAD = 1
+LAG_PRODUCT = 2 + AHEAD
+LAG_NORMALISE = LAG_PRODUCT + 1
 LAG_GATE = LAG_NORMALISE + PAIR
 LAG_BACK_F = LAG_GATE + 1
 LAG_KEEP = LAG_BACK_F + 1
-LAG_BACK_O = LAG_GATE + PAIR
 LAG_TANH = LAG_KEEP + 1
 LAG_OUT = LAG_TANH
+LAG_BACK_O = LAG_OUT
+CONST_STEP = 1
 
 
 def tile_layernormlstmcell_pb_t_kernel(
@@ -85,6 +84,10 @@ def tile_layernormlstmcell_pb_t_kernel(
             nc.sync.dma_start(out=ic_sb[k][:], in_=ic_rows[:, tiles_of(k), :])
 
         load_x_h(0)
+        vectors = const.tile([P, FEATURES], BF16)
+        nc.vector.memset(vectors[:], 0.0)
+        for v, vector in enumerate((lnf_g, lnf_b, lno_g, lno_b, Wf_b, Wo_b)):
+            nc.scalar.dma_start(out=vectors[v : v + 1, :], in_=vector.unsqueeze(0))
 
         weights = ((Wf_w_words, Wf_w_scales), (Uf_w_words, Uf_w_scales),
                    (Wo_w_words, Wo_w_scales), (Uo_w_words, Uo_w_scales))
@@ -111,25 +114,23 @@ def tile_layernormlstmcell_pb_t_kernel(
         neg_half = const.tile([P, 2], F32)
         nc.vector.memset(neg_half[:], -0.5)
 
-        vectors = const.tile([P, FEATURES], BF16)
-        nc.vector.memset(vectors[:], 0.0)
-        for v, vector in enumerate((lnf_g, lnf_b, lno_g, lno_b, Wf_b, Wo_b)):
-            nc.scalar.dma_start(out=vectors[v : v + 1, :], in_=vector.unsqueeze(0))
-        columns = psum.tile([P, BLOCKS, P], BF16, name="columns", tag="turned")
-        for j in range(BLOCKS):
-            nc.tensor.transpose(columns[:, j, :], vectors[:, j * P : (j + 1) * P], ident_bf[:])
         affine = const.tile([P, BLOCKS, 4], F32)
-        nc.vector.tensor_copy(out=affine[:], in_=columns[:, :, 0:4])
         bias = const.tile([P, 2, FEATURES], BF16)
-        for gate in range(2):
-            spread = psum.tile([P, FEATURES], F32, name="spread", tag="pre", bufs=3)
-            nc.tensor.matmul(spread[:], lhsT=ident_bf[:, 4 + gate : 5 + gate].to_broadcast([P, P]),
-                             rhs=vectors[:], start=True, stop=True)
-            nc.vector.tensor_copy(out=bias[:, gate, :], in_=spread[:])
+
+        def spread_constants():
+            columns = psum.tile([P, BLOCKS, P], BF16, name="columns", tag="back_f")
+            for j in range(BLOCKS):
+                nc.tensor.transpose(columns[:, j, :], vectors[:, j * P : (j + 1) * P], ident_bf[:])
+            nc.vector.tensor_copy(out=affine[:], in_=columns[:, :, 0:4])
+            for gate in range(2):
+                spread = psum.tile([P, FEATURES], F32, name="spread", tag=("normed_t_low", "normed_t_high")[gate])
+                nc.tensor.matmul(spread[:], lhsT=ident_bf[:, 4 + gate : 5 + gate].to_broadcast([P, P]),
+                                 rhs=vectors[:], start=True, stop=True)
+                nc.vector.tensor_copy(out=bias[:, gate, :], in_=spread[:])
 
         def turn(t):
             k, i = divmod(t, PAIR)
-            turned[t] = psum.tile([P, 2, 2, P], F32, name="turned")
+            turned[t] = psum.tile([P, 2, 2, P], F32, name="turned", bufs=2)
             for a, source in enumerate((x_sb[k], h_sb[k])):
                 words = source[:, i, :].bitcast(F32)
                 for u in range(2):
@@ -140,33 +141,31 @@ def tile_layernormlstmcell_pb_t_kernel(
             nc.scalar.copy(out=grouped[t][:].bitcast(F32), in_=turned[t][:].rearrange("p a u r -> p a r u"))
 
         def quantise(t):
-            xh_codes[t] = work.tile([P, 2 * P], U32, name="xh_codes", align_bytes=64)
-            xh_scales[t] = work.tile([P, 2 * P], U8, name="xh_scales", align_bytes=64)
+            xh_codes[t] = work.tile([P, 2 * P], U32, name="xh_codes", align_bytes=64, bufs=AHEAD + 3)
+            xh_scales[t] = work.tile([P, 2 * P], U8, name="xh_scales", align_bytes=64, bufs=AHEAD + 3)
             nc.vector.quantize_mx(
                 out=xh_codes[t][:].bitcast(FP8X4),
                 scales=xh_scales[t][:],
                 in_=grouped[t][:].rearrange("p a r t -> p (a r t)"),
             )
 
-        def products(t, a):
-            if a == 0:
-                pre[t] = [psum.tile([P, FEATURES], F32, name="pre_f", tag="pre", bufs=3),
-                          psum.tile([P, FEATURES], F32, name="pre_o", tag="pre", bufs=3)]
+        def products(t):
+            pre[t] = [psum.tile([P, FEATURES], F32, name="pre_f"), psum.tile([P, FEATURES], F32, name="pre_o")]
             for gate in range(2):
-                w = 2 * gate + a
-                nc.tensor.matmul_mx(
-                    out=pre[t][gate][:],
-                    lhsT=xh_codes[t][:, a * P : (a + 1) * P].bitcast(FP8X4),
-                    lhsT_scale=xh_scales[t][:, a * P : (a + 1) * P],
-                    rhs=w_codes[:, w, :].bitcast(FP8X4),
-                    rhs_scale=w_scales[:, w, :],
-                    start=(a == 0),
-                    stop=(a == 1),
-                )
+                for a in range(2):
+                    w = 2 * gate + a
+                    nc.tensor.matmul_mx(
+                        out=pre[t][gate][:],
+                        lhsT=xh_codes[t][:, a * P : (a + 1) * P].bitcast(FP8X4),
+                        lhsT_scale=xh_scales[t][:, a * P : (a + 1) * P],
+                        rhs=w_codes[:, w, :].bitcast(FP8X4),
+                        rhs_scale=w_scales[:, w, :],
+                        start=(a == 0),
+                        stop=(a == 1),
+                    )
 
         def add_bias(t):
-            y[t] = [work.tile([P, FEATURES], F32, name="y_f", bufs=4),
-                    work.tile([P, FEATURES], F32, name="y_o", bufs=4)]
+            y[t] = [work.tile([P, FEATURES], F32, name="y_f"), work.tile([P, FEATURES], F32, name="y_o")]
             row_sum[t] = small.tile([P, 2], F32, name="row_sum")
             for gate in range(2):
                 nc.vector.scalar_tensor_tensor(
@@ -174,24 +173,22 @@ def tile_layernormlstmcell_pb_t_kernel(
                     op0=ALU.mult, op1=ALU.add, accum_out=row_sum[t][:, gate : gate + 1],
                 )
 
-        def mean(t):
-            neg_mean[t] = small.tile([P, 2], F32, name="neg_mean")
-            nc.vector.tensor_scalar_mul(out=neg_mean[t][:], in0=row_sum[t][:], scalar1=-1.0 / FEATURES)
-
         def squares(t):
             sum_sq[t] = small.tile([P, 2], F32, name="sum_sq")
             for gate in range(2):
                 unused = work.tile([P, FEATURES], BF16, name="unused")
                 nc.scalar.activation(
                     out=unused[:], in_=y[t][gate][:], func=ACT.Square,
-                    bias=neg_mean[t][:, gate : gate + 1], scale=1.0,
+                    bias=row_sum[t][:, gate : gate + 1], scale=-1.0 * FEATURES,
                     accum_out=sum_sq[t][:, gate : gate + 1],
                 )
 
         def variance(t):
             var_eps[t] = small.tile([P, 2], F32, name="var_eps")
-            nc.vector.tensor_scalar(out=var_eps[t][:], in0=sum_sq[t][:], scalar1=1.0 / FEATURES,
+            nc.vector.tensor_scalar(out=var_eps[t][:], in0=sum_sq[t][:], scalar1=1.0 / FEATURES ** 3,
                                     scalar2=EPS, op0=ALU.mult, op1=ALU.add)
+            neg_mean[t] = small.tile([P, 2], F32, name="neg_mean")
+            nc.vector.tensor_scalar_mul(out=neg_mean[t][:], in0=row_sum[t][:], scalar1=-1.0 / FEATURES)
 
         def inverse_deviation(t):
             rstd[t] = small.tile([P, 2], F32, name="rstd")
@@ -268,44 +265,42 @@ def tile_layernormlstmcell_pb_t_kernel(
                 if 0 <= (step - LAG_KEEP) // PAIR + LOAD_AHEAD < PAIRS:
                     load_c_ic((step - LAG_KEEP) // PAIR + LOAD_AHEAD)
 
+            if step == CONST_STEP:
+                spread_constants()
             if due(step, LAG_KEEP):
                 keep(step - LAG_KEEP)
             if due(step, LAG_NORMALISE):
                 inverse_deviation(step - LAG_NORMALISE)
             if due(step, LAG_KEEP):
                 add_input(step - LAG_KEEP)
+            if due(step, LAG_PRODUCT):
+                products(step - LAG_PRODUCT)
             if due(step, LAG_TANH):
                 squash(step - LAG_TANH)
-            if due(step, LAG_BIAS):
-                add_bias(step - LAG_BIAS)
             if due(step, LAG_PRODUCT):
-                products(step - LAG_PRODUCT, 0)
+                add_bias(step - LAG_PRODUCT)
+            if due(step, LAG_BACK_O):
+                turn_back(step - LAG_BACK_O, OUTPUT)
             if due(step, LAG_OUT):
                 put_out(step - LAG_OUT)
-            if due(step, LAG_BACK_F):
-                turn_back(step - LAG_BACK_F, FORGET)
+            if due(step, LAG_QUANTISE):
+                regroup(step - LAG_QUANTISE)
+            if due(step, LAG_PRODUCT):
+                squares(step - LAG_PRODUCT)
+            if due(step, 0):
+                turn(step)
             if due(step, LAG_GATE):
                 turn_normed((step - LAG_GATE) // PAIR, (step - LAG_GATE) % PAIR)
-            if due(step, LAG_REGROUP):
-                regroup(step - LAG_REGROUP)
-            if due(step, LAG_SQUARES):
-                squares(step - LAG_SQUARES)
-            if due(step, LAG_BIAS):
-                mean(step - LAG_BIAS)
             if due(step, LAG_NORMALISE):
                 normalise(step - LAG_NORMALISE)
-            if due(step, LAG_PRODUCT):
-                products(step - LAG_PRODUCT, 1)
             if due(step, LAG_GATE):
                 sigmoids((step - LAG_GATE) // PAIR, (step - LAG_GATE) % PAIR)
             if due(step, LAG_QUANTISE):
                 quantise(step - LAG_QUANTISE)
-            if due(step, LAG_SQUARES):
-                variance(step - LAG_SQUARES)
-            if due(step, LAG_BACK_O):
-                turn_back(step - LAG_BACK_O, OUTPUT)
-            if due(step, 0):
-                turn(step)
+            if due(step, LAG_PRODUCT):
+                variance(step - LAG_PRODUCT)
+            if due(step, LAG_BACK_F):
+                turn_back(step - LAG_BACK_F, FORGET)
 
             if due(step, LAG_KEEP) and (step - LAG_KEEP) % PAIR == PAIR - 1:
                 k = (step - LAG_KEEP) // PAIR

@@ -71,11 +71,11 @@ def tile_layernormlstmcell_pb_t_kernel(
         def tiles_of(k):
             return slice(k * PAIR, (k + 1) * PAIR)
 
-        def load_x_h(k):
+        def load_x_h(k, queue):
             x_sb[k] = loads.tile([P, PAIR, FEATURES], BF16, name="x_sb")
             h_sb[k] = loads.tile([P, PAIR, FEATURES], BF16, name="h_sb")
-            nc.sync.dma_start(out=x_sb[k][:], in_=x_rows[:, tiles_of(k), :])
-            nc.sync.dma_start(out=h_sb[k][:], in_=h_rows[:, tiles_of(k), :])
+            queue.dma_start(out=x_sb[k][:], in_=x_rows[:, tiles_of(k), :])
+            queue.dma_start(out=h_sb[k][:], in_=h_rows[:, tiles_of(k), :])
 
         def load_c_ic(k):
             c_sb[k] = loads.tile([P, PAIR, FEATURES], BF16, name="c_sb")
@@ -83,29 +83,34 @@ def tile_layernormlstmcell_pb_t_kernel(
             nc.sync.dma_start(out=c_sb[k][:], in_=c_rows[:, tiles_of(k), :])
             nc.sync.dma_start(out=ic_sb[k][:], in_=ic_rows[:, tiles_of(k), :])
 
-        load_x_h(0)
-        vectors = const.tile([P, FEATURES], BF16)
-        nc.vector.memset(vectors[:], 0.0)
-        for v, vector in enumerate((lnf_g, lnf_b, lno_g, lno_b, Wf_b, Wo_b)):
-            nc.scalar.dma_start(out=vectors[v : v + 1, :], in_=vector.unsqueeze(0))
-
         weights = ((Wf_w_words, Wf_w_scales), (Uf_w_words, Uf_w_scales),
                    (Wo_w_words, Wo_w_scales), (Uo_w_words, Uo_w_scales))
         w_codes = const.tile([P, 4, 4 * FEATURES], U8, align_bytes=64)
         w_scales = const.tile([P, 4, FEATURES], U8, align_bytes=64)
+        vectors = const.tile([P, FEATURES], BF16)
+        nc.vector.memset(vectors[:], 0.0)
         nc.vector.memset(w_scales[:].bitcast(I32), 0)
+
+        def load_codes(w):
+            nc.scalar.dma_start(
+                out=w_codes[:, w, :].bitcast(F32),
+                in_=weights[w][0].rearrange("g p n t -> (g p) (n t)").bitcast(F32),
+            )
+
+        load_x_h(0, nc.scalar)
+        for v, vector in enumerate((lnf_g, lnf_b, lno_g, lno_b, Wf_b, Wo_b)):
+            nc.scalar.dma_start(out=vectors[v : v + 1, :], in_=vector.unsqueeze(0))
         for w, (code_bytes, scale_bytes) in enumerate(weights):
             for quadrant in range(4):
                 nc.sync.dma_start(
                     out=w_scales[32 * quadrant : 32 * quadrant + 4, w, :].bitcast(I32),
                     in_=scale_bytes[0, 4 * quadrant : 4 * quadrant + 4, :].bitcast(I32),
                 )
-        for w, (code_bytes, scale_bytes) in enumerate(weights):
-            nc.sync.dma_start(
-                out=w_codes[:, w, :].bitcast(I32),
-                in_=code_bytes.rearrange("g p n t -> (g p) (n t)").bitcast(I32),
-            )
-        load_x_h(1)
+        load_codes(0)
+        load_codes(1)
+        load_x_h(1, nc.scalar)
+        load_codes(2)
+        load_codes(3)
 
         ident = const.tile([P, P], F32)
         make_identity(nc, ident[:])
@@ -126,7 +131,7 @@ def tile_layernormlstmcell_pb_t_kernel(
                 spread = psum.tile([P, FEATURES], F32, name="spread", tag=("normed_t_low", "normed_t_high")[gate])
                 nc.tensor.matmul(spread[:], lhsT=ident_bf[:, 4 + gate : 5 + gate].to_broadcast([P, P]),
                                  rhs=vectors[:], start=True, stop=True)
-                nc.vector.tensor_copy(out=bias[:, gate, :], in_=spread[:])
+                nc.scalar.copy(out=bias[:, gate, :], in_=spread[:])
 
         def turn(t):
             k, i = divmod(t, PAIR)
@@ -260,13 +265,11 @@ def tile_layernormlstmcell_pb_t_kernel(
         for step in range(ROW_TILES + LAG_OUT + 1):
             if step % PAIR == 0:
                 if step // PAIR + LOAD_AHEAD < PAIRS:
-                    load_x_h(step // PAIR + LOAD_AHEAD)
+                    load_x_h(step // PAIR + LOAD_AHEAD, nc.sync)
             if (step - LAG_KEEP) % PAIR == 0:
                 if 0 <= (step - LAG_KEEP) // PAIR + LOAD_AHEAD < PAIRS:
                     load_c_ic((step - LAG_KEEP) // PAIR + LOAD_AHEAD)
 
-            if step == CONST_STEP:
-                spread_constants()
             if due(step, LAG_KEEP):
                 keep(step - LAG_KEEP)
             if due(step, LAG_NORMALISE):
@@ -301,6 +304,8 @@ def tile_layernormlstmcell_pb_t_kernel(
                 variance(step - LAG_PRODUCT)
             if due(step, LAG_BACK_F):
                 turn_back(step - LAG_BACK_F, FORGET)
+            if step == CONST_STEP:
+                spread_constants()
 
             if due(step, LAG_KEEP) and (step - LAG_KEEP) % PAIR == PAIR - 1:
                 k = (step - LAG_KEEP) // PAIR

@@ -27,15 +27,18 @@ FLOPS = 4 * 2 * ROWS * FEATURES * FEATURES
 FORGET, OUTPUT = 0, 1
 
 LAG_QUANTISE = 1
+SQ_LATER = 1
 AHEAD = 1
 LAG_PRODUCT = 2 + AHEAD
-LAG_NORMALISE = LAG_PRODUCT + 1
+LAG_SQUARES = LAG_PRODUCT + SQ_LATER
+LAG_NORMALISE = LAG_SQUARES + 1
 LAG_GATE = LAG_NORMALISE + PAIR
 LAG_BACK_F = LAG_GATE + 1
 LAG_KEEP = LAG_BACK_F + 1
 LAG_TANH = LAG_KEEP + 1
 LAG_OUT = LAG_TANH
 LAG_BACK_O = LAG_OUT
+VECTOR_EVERY = 4
 CONST_STEP = 1
 
 
@@ -88,36 +91,33 @@ def tile_layernormlstmcell_pb_t_kernel(
         w_codes = const.tile([P, 4, 4 * FEATURES], U8, align_bytes=64)
         w_scales = const.tile([P, 4, FEATURES], U8, align_bytes=64)
         vectors = const.tile([P, FEATURES], BF16)
+        neg_half = const.tile([P, 2], F32)
+        warm = const.tile([P, 2], F32)
+        nc.vector.memset(neg_half[:], -0.5)
         nc.vector.memset(vectors[:], 0.0)
         nc.vector.memset(w_scales[:].bitcast(I32), 0)
 
-        def load_codes(w):
-            nc.scalar.dma_start(
-                out=w_codes[:, w, :].bitcast(F32),
-                in_=weights[w][0].rearrange("g p n t -> (g p) (n t)").bitcast(F32),
-            )
-
-        load_x_h(0, nc.scalar)
+        load_x_h(0, nc.sync)
+        load_x_h(1, nc.sync)
         for v, vector in enumerate((lnf_g, lnf_b, lno_g, lno_b, Wf_b, Wo_b)):
-            nc.scalar.dma_start(out=vectors[v : v + 1, :], in_=vector.unsqueeze(0))
+            nc.sync.dma_start(out=vectors[v : v + 1, :], in_=vector.unsqueeze(0))
         for w, (code_bytes, scale_bytes) in enumerate(weights):
             for quadrant in range(4):
                 nc.sync.dma_start(
                     out=w_scales[32 * quadrant : 32 * quadrant + 4, w, :].bitcast(I32),
                     in_=scale_bytes[0, 4 * quadrant : 4 * quadrant + 4, :].bitcast(I32),
                 )
-        load_codes(0)
-        load_codes(1)
-        load_x_h(1, nc.scalar)
-        load_codes(2)
-        load_codes(3)
+        nc.scalar.activation(out=warm[:], in_=neg_half[:], func=ACT.Sigmoid)
+        for w, (code_bytes, scale_bytes) in enumerate(weights):
+            nc.scalar.dma_start(
+                out=w_codes[:, w, :].bitcast(F32),
+                in_=code_bytes.rearrange("g p n t -> (g p) (n t)").bitcast(F32),
+            )
 
         ident = const.tile([P, P], F32)
         make_identity(nc, ident[:])
         ident_bf = const.tile([P, P], BF16)
         make_identity(nc, ident_bf[:])
-        neg_half = const.tile([P, 2], F32)
-        nc.vector.memset(neg_half[:], -0.5)
 
         affine = const.tile([P, BLOCKS, 4], F32)
         bias = const.tile([P, 2, FEATURES], BF16)
@@ -131,7 +131,7 @@ def tile_layernormlstmcell_pb_t_kernel(
                 spread = psum.tile([P, FEATURES], F32, name="spread", tag=("normed_t_low", "normed_t_high")[gate])
                 nc.tensor.matmul(spread[:], lhsT=ident_bf[:, 4 + gate : 5 + gate].to_broadcast([P, P]),
                                  rhs=vectors[:], start=True, stop=True)
-                nc.scalar.copy(out=bias[:, gate, :], in_=spread[:])
+                nc.vector.tensor_copy(out=bias[:, gate, :], in_=spread[:])
 
         def turn(t):
             k, i = divmod(t, PAIR)
@@ -143,7 +143,10 @@ def tile_layernormlstmcell_pb_t_kernel(
 
         def regroup(t):
             grouped[t] = work.tile([P, 2, P, 4], BF16, name="grouped", align_bytes=64)
-            nc.scalar.copy(out=grouped[t][:].bitcast(F32), in_=turned[t][:].rearrange("p a u r -> p a r u"))
+            if t % VECTOR_EVERY == VECTOR_EVERY - 1:
+                nc.vector.tensor_copy(out=grouped[t][:].bitcast(F32), in_=turned[t][:].rearrange("p a u r -> p a r u"))
+            else:
+                nc.scalar.copy(out=grouped[t][:].bitcast(F32), in_=turned[t][:].rearrange("p a u r -> p a r u"))
 
         def quantise(t):
             xh_codes[t] = work.tile([P, 2 * P], U32, name="xh_codes", align_bytes=64, bufs=AHEAD + 3)
@@ -170,7 +173,7 @@ def tile_layernormlstmcell_pb_t_kernel(
                     )
 
         def add_bias(t):
-            y[t] = [work.tile([P, FEATURES], F32, name="y_f"), work.tile([P, FEATURES], F32, name="y_o")]
+            y[t] = [work.tile([P, FEATURES], F32, name="y_f", bufs=4), work.tile([P, FEATURES], F32, name="y_o", bufs=4)]
             row_sum[t] = small.tile([P, 2], F32, name="row_sum")
             for gate in range(2):
                 nc.vector.scalar_tensor_tensor(
@@ -288,8 +291,8 @@ def tile_layernormlstmcell_pb_t_kernel(
                 put_out(step - LAG_OUT)
             if due(step, LAG_QUANTISE):
                 regroup(step - LAG_QUANTISE)
-            if due(step, LAG_PRODUCT):
-                squares(step - LAG_PRODUCT)
+            if due(step, LAG_SQUARES):
+                squares(step - LAG_SQUARES)
             if due(step, 0):
                 turn(step)
             if due(step, LAG_GATE):
@@ -300,8 +303,8 @@ def tile_layernormlstmcell_pb_t_kernel(
                 sigmoids((step - LAG_GATE) // PAIR, (step - LAG_GATE) % PAIR)
             if due(step, LAG_QUANTISE):
                 quantise(step - LAG_QUANTISE)
-            if due(step, LAG_PRODUCT):
-                variance(step - LAG_PRODUCT)
+            if due(step, LAG_SQUARES):
+                variance(step - LAG_SQUARES)
             if due(step, LAG_BACK_F):
                 turn_back(step - LAG_BACK_F, FORGET)
             if step == CONST_STEP:

@@ -38,7 +38,7 @@ LAG_KEEP = LAG_BACK_F + 1
 LAG_TANH = LAG_KEEP + 1
 LAG_OUT = LAG_TANH
 LAG_BACK_O = LAG_OUT
-VECTOR_EVERY = 4
+VECTOR_EVERY = 0
 CONST_STEP = 1
 
 
@@ -143,7 +143,7 @@ def tile_layernormlstmcell_pb_t_kernel(
 
         def regroup(t):
             grouped[t] = work.tile([P, 2, P, 4], BF16, name="grouped", align_bytes=64)
-            if t % VECTOR_EVERY == VECTOR_EVERY - 1:
+            if VECTOR_EVERY > 0 and t % VECTOR_EVERY == VECTOR_EVERY - 1:
                 nc.vector.tensor_copy(out=grouped[t][:].bitcast(F32), in_=turned[t][:].rearrange("p a u r -> p a r u"))
             else:
                 nc.scalar.copy(out=grouped[t][:].bitcast(F32), in_=turned[t][:].rearrange("p a u r -> p a r u"))
@@ -195,8 +195,11 @@ def tile_layernormlstmcell_pb_t_kernel(
             var_eps[t] = small.tile([P, 2], F32, name="var_eps")
             nc.vector.tensor_scalar(out=var_eps[t][:], in0=sum_sq[t][:], scalar1=1.0 / FEATURES ** 3,
                                     scalar2=EPS, op0=ALU.mult, op1=ALU.add)
+
+        def negative_mean(t):
             neg_mean[t] = small.tile([P, 2], F32, name="neg_mean")
-            nc.vector.tensor_scalar_mul(out=neg_mean[t][:], in0=row_sum[t][:], scalar1=-1.0 / FEATURES)
+            nc.gpsimd.tensor_scalar(out=neg_mean[t][:], in0=row_sum[t][:], scalar1=-1.0 / FEATURES, scalar2=0.0,
+                                    op0=ALU.mult, op1=ALU.add)
 
         def inverse_deviation(t):
             rstd[t] = small.tile([P, 2], F32, name="rstd")
@@ -279,6 +282,8 @@ def tile_layernormlstmcell_pb_t_kernel(
                 inverse_deviation(step - LAG_NORMALISE)
             if due(step, LAG_KEEP):
                 add_input(step - LAG_KEEP)
+            if due(step, LAG_SQUARES):
+                negative_mean(step - LAG_SQUARES)
             if due(step, LAG_PRODUCT):
                 products(step - LAG_PRODUCT)
             if due(step, LAG_TANH):

from contextlib import ExitStack

import concourse.mybir as mybir
from concourse.masks import make_identity

F32 = mybir.dt.float32
BF16 = mybir.dt.bfloat16
I32 = mybir.dt.int32
U8 = mybir.dt.uint8
U32 = mybir.dt.uint32
FP8X4 = mybir.dt.float8_e4m3fn_x4
ALU = mybir.AluOpType
ACT = mybir.ActivationFunctionType

P = 128
ROWS = 4096
FEATURES = 512
ROW_TILES = ROWS // P
BLOCKS = FEATURES // P
PAIR = 2
PAIRS = ROW_TILES // PAIR
LOAD_AHEAD = 2
WORDS = FEATURES // 2
EPS = 1e-5
FLOPS = 4 * 2 * ROWS * FEATURES * FEATURES

FORGET, OUTPUT = 0, 1

LAG_QUANTISE = 1
SQ_LATER = 1
AHEAD = 1
LAG_PRODUCT = 2 + AHEAD
LAG_SQUARES = LAG_PRODUCT + SQ_LATER
LAG_NORMALISE = LAG_SQUARES + 1
LAG_GATE = LAG_NORMALISE + PAIR
LAG_BACK_F = LAG_GATE + 1
LAG_KEEP = LAG_BACK_F + 1
LAG_TANH = LAG_KEEP + 1
LAG_OUT = LAG_TANH
LAG_BACK_O = LAG_OUT
VECTOR_EVERY = 0
CONST_STEP = 1


def tile_layernormlstmcell_pb_t_kernel(
    tc, x, h, c, ic_tilde,
    Wf_w_words, Wf_w_scales, Wf_b, Uf_w_words, Uf_w_scales, lnf_g, lnf_b,
    Wo_w_words, Wo_w_scales, Wo_b, Uo_w_words, Uo_w_scales, lno_g, lno_b,
    out_0, out_1,
):
    nc = tc.nc
    x_rows = x.rearrange("(p t) k -> p t k", t=ROW_TILES)
    h_rows = h.rearrange("(p t) k -> p t k", t=ROW_TILES)
    c_rows = c.rearrange("(p t) k -> p t k", t=ROW_TILES)
    ic_rows = ic_tilde.rearrange("(p t) k -> p t k", t=ROW_TILES)
    h_new_rows = out_0.rearrange("(p t) k -> p t k", t=ROW_TILES)
    c_new_rows = out_1.rearrange("(p t) k -> p t k", t=ROW_TILES)

    with ExitStack() as ctx:
        const = ctx.enter_context(tc.tile_pool(name="const", bufs=1))
        loads = ctx.enter_context(tc.tile_pool(name="loads", bufs=LOAD_AHEAD + 1))
        stores = ctx.enter_context(tc.tile_pool(name="stores", bufs=3))
        work = ctx.enter_context(tc.tile_pool(name="work", bufs=3))
        pairs = ctx.enter_context(tc.tile_pool(name="pairs", bufs=2))
        small = ctx.enter_context(tc.tile_pool(name="small", bufs=4))
        psum = ctx.enter_context(tc.psum_pool(name="psum", bufs=1))
        ctx.enter_context(tc.manual_schedule())

        x_sb, h_sb, c_sb, ic_sb, c_new, h_new = {}, {}, {}, {}, {}, {}
        turned, grouped, xh_codes, xh_scales, pre, y = {}, {}, {}, {}, {}, {}
        row_sum, neg_mean, sum_sq, var_eps, rstd = {}, {}, {}, {}, {}
        normed, normed_t, gate_t, back, kept, squashed = {}, {}, {}, {}, {}, {}

        def tiles_of(k):
            return slice(k * PAIR, (k + 1) * PAIR)

        def load_x_h(k, queue):
            x_sb[k] = loads.tile([P, PAIR, FEATURES], BF16, name="x_sb")
            h_sb[k] = loads.tile([P, PAIR, FEATURES], BF16, name="h_sb")
            queue.dma_start(out=x_sb[k][:], in_=x_rows[:, tiles_of(k), :])
            queue.dma_start(out=h_sb[k][:], in_=h_rows[:, tiles_of(k), :])

        def load_c_ic(k):
            c_sb[k] = loads.tile([P, PAIR, FEATURES], BF16, name="c_sb")
            ic_sb[k] = loads.tile([P, PAIR, FEATURES], BF16, name="ic_sb")
            nc.sync.dma_start(out=c_sb[k][:], in_=c_rows[:, tiles_of(k), :])
            nc.sync.dma_start(out=ic_sb[k][:], in_=ic_rows[:, tiles_of(k), :])

        weights = ((Wf_w_words, Wf_w_scales), (Uf_w_words, Uf_w_scales),
                   (Wo_w_words, Wo_w_scales), (Uo_w_words, Uo_w_scales))
        w_codes = const.tile([P, 4, 4 * FEATURES], U8, align_bytes=64)
        w_scales = const.tile([P, 4, FEATURES], U8, align_bytes=64)
        vectors = const.tile([P, FEATURES], BF16)
        neg_half = const.tile([P, 2], F32)
        warm = const.tile([P, 2], F32)
        nc.vector.memset(neg_half[:], -0.5)
        nc.vector.memset(vectors[:], 0.0)
        nc.vector.memset(w_scales[:].bitcast(I32), 0)

        load_x_h(0, nc.sync)
        load_x_h(1, nc.sync)
        for v, vector in enumerate((lnf_g, lnf_b, lno_g, lno_b, Wf_b, Wo_b)):
            nc.sync.dma_start(out=vectors[v : v + 1, :], in_=vector.unsqueeze(0))
        for w, (code_bytes, scale_bytes) in enumerate(weights):
            for quadrant in range(4):
                nc.sync.dma_start(
                    out=w_scales[32 * quadrant : 32 * quadrant + 4, w, :].bitcast(I32),
                    in_=scale_bytes[0, 4 * quadrant : 4 * quadrant + 4, :].bitcast(I32),
                )
        nc.scalar.activation(out=warm[:], in_=neg_half[:], func=ACT.Sigmoid)
        for w, (code_bytes, scale_bytes) in enumerate(weights):
            nc.scalar.dma_start(
                out=w_codes[:, w, :].bitcast(F32),
                in_=code_bytes.rearrange("g p n t -> (g p) (n t)").bitcast(F32),
            )

        ident = const.tile([P, P], F32)
        make_identity(nc, ident[:])
        ident_bf = const.tile([P, P], BF16)
        make_identity(nc, ident_bf[:])

        affine = const.tile([P, BLOCKS, 4], F32)
        bias = const.tile([P, 2, FEATURES], BF16)

        def spread_constants():
            columns = psum.tile([P, BLOCKS, P], BF16, name="columns", tag="back_f")
            for j in range(BLOCKS):
                nc.tensor.transpose(columns[:, j, :], vectors[:, j * P : (j + 1) * P], ident_bf[:])
            nc.vector.tensor_copy(out=affine[:], in_=columns[:, :, 0:4])
            for gate in range(2):
                spread = psum.tile([P, FEATURES], F32, name="spread", tag=("normed_t_low", "normed_t_high")[gate])
                nc.tensor.matmul(spread[:], lhsT=ident_bf[:, 4 + gate : 5 + gate].to_broadcast([P, P]),
                                 rhs=vectors[:], start=True, stop=True)
                nc.vector.tensor_copy(out=bias[:, gate, :], in_=spread[:])

        def turn(t):
            k, i = divmod(t, PAIR)
            turned[t] = psum.tile([P, 2, 2, P], F32, name="turned", bufs=2)
            for a, source in enumerate((x_sb[k], h_sb[k])):
                words = source[:, i, :].bitcast(F32)
                for u in range(2):
                    nc.tensor.transpose(turned[t][:, a, u, :], words[:, u:WORDS:2], ident[:])

        def regroup(t):
            grouped[t] = work.tile([P, 2, P, 4], BF16, name="grouped", align_bytes=64)
            if VECTOR_EVERY > 0 and t % VECTOR_EVERY == VECTOR_EVERY - 1:
                nc.vector.tensor_copy(out=grouped[t][:].bitcast(F32), in_=turned[t][:].rearrange("p a u r -> p a r u"))
            else:
                nc.scalar.copy(out=grouped[t][:].bitcast(F32), in_=turned[t][:].rearrange("p a u r -> p a r u"))

        def quantise(t):
            xh_codes[t] = work.tile([P, 2 * P], U32, name="xh_codes", align_bytes=64, bufs=AHEAD + 3)
            xh_scales[t] = work.tile([P, 2 * P], U8, name="xh_scales", align_bytes=64, bufs=AHEAD + 3)
            nc.vector.quantize_mx(
                out=xh_codes[t][:].bitcast(FP8X4),
                scales=xh_scales[t][:],
                in_=grouped[t][:].rearrange("p a r t -> p (a r t)"),
            )

        def products(t):
            pre[t] = [psum.tile([P, FEATURES], F32, name="pre_f"), psum.tile([P, FEATURES], F32, name="pre_o")]
            for gate in range(2):
                for a in range(2):
                    w = 2 * gate + a
                    nc.tensor.matmul_mx(
                        out=pre[t][gate][:],
                        lhsT=xh_codes[t][:, a * P : (a + 1) * P].bitcast(FP8X4),
                        lhsT_scale=xh_scales[t][:, a * P : (a + 1) * P],
                        rhs=w_codes[:, w, :].bitcast(FP8X4),
                        rhs_scale=w_scales[:, w, :],
                        start=(a == 0),
                        stop=(a == 1),
                    )

        def add_bias(t):
            y[t] = [work.tile([P, FEATURES], F32, name="y_f", bufs=4), work.tile([P, FEATURES], F32, name="y_o", bufs=4)]
            row_sum[t] = small.tile([P, 2], F32, name="row_sum")
            for gate in range(2):
                nc.vector.scalar_tensor_tensor(
                    out=y[t][gate][:], in0=pre[t][gate][:], scalar=1.0, in1=bias[:, gate, :],
                    op0=ALU.mult, op1=ALU.add, accum_out=row_sum[t][:, gate : gate + 1],
                )

        def squares(t):
            sum_sq[t] = small.tile([P, 2], F32, name="sum_sq")
            for gate in range(2):
                unused = work.tile([P, FEATURES], BF16, name="unused")
                nc.scalar.activation(
                    out=unused[:], in_=y[t][gate][:], func=ACT.Square,
                    bias=row_sum[t][:, gate : gate + 1], scale=-1.0 * FEATURES,
                    accum_out=sum_sq[t][:, gate : gate + 1],
                )

        def variance(t):
            var_eps[t] = small.tile([P, 2], F32, name="var_eps")
            nc.vector.tensor_scalar(out=var_eps[t][:], in0=sum_sq[t][:], scalar1=1.0 / FEATURES ** 3,
                                    scalar2=EPS, op0=ALU.mult, op1=ALU.add)

        def negative_mean(t):
            neg_mean[t] = small.tile([P, 2], F32, name="neg_mean")
            nc.gpsimd.tensor_scalar(out=neg_mean[t][:], in0=row_sum[t][:], scalar1=-1.0 / FEATURES, scalar2=0.0,
                                    op0=ALU.mult, op1=ALU.add)

        def inverse_deviation(t):
            rstd[t] = small.tile([P, 2], F32, name="rstd")
            nc.gpsimd.tensor_tensor(out=rstd[t][:], in0=var_eps[t][:], in1=neg_half[:], op=ALU.pow)

        def normalise(t):
            k, i = divmod(t, PAIR)
            if i == 0:
                normed[k] = [pairs.tile([P, PAIR, FEATURES], F32, name="normed_f"),
                             pairs.tile([P, PAIR, FEATURES], F32, name="normed_o")]
            for gate in range(2):
                nc.vector.tensor_scalar(
                    out=normed[k][gate][:, i, :], in0=y[t][gate][:],
                    scalar1=neg_mean[t][:, gate : gate + 1], scalar2=rstd[t][:, gate : gate + 1],
                    op0=ALU.add, op1=ALU.mult,
                )

        def turn_normed(k, gate):
            normed_t[k, gate] = [psum.tile([P, 2, PAIR, P], F32, name="normed_t_low"),
                                 psum.tile([P, 2, PAIR, P], F32, name="normed_t_high")]
            for j in range(BLOCKS):
                for i in range(PAIR):
                    nc.tensor.transpose(normed_t[k, gate][j // 2][:, j % 2, i, :],
                                        normed[k][gate][:, i, j * P : (j + 1) * P], ident[:])

        def sigmoids(k, gate):
            gate_t[k, gate] = pairs.tile([P, BLOCKS, PAIR * P], F32, name=("gate_t_f", "gate_t_o")[gate])
            for j in range(BLOCKS):
                nc.scalar.activation(
                    out=gate_t[k, gate][:, j, :],
                    in_=normed_t[k, gate][j // 2][:, j % 2, :, :].rearrange("p i r -> p (i r)"),
                    func=ACT.Sigmoid,
                    scale=affine[:, j, 2 * gate : 2 * gate + 1],
                    bias=affine[:, j, 2 * gate + 1 : 2 * gate + 2],
                )

        def turn_back(t, gate):
            k, i = divmod(t, PAIR)
            back[t, gate] = psum.tile([P, FEATURES], F32, name=("back_f", "back_o")[gate])
            for j in range(BLOCKS):
                nc.tensor.transpose(back[t, gate][:, j * P : (j + 1) * P],
                                    gate_t[k, gate][:, j, i * P : (i + 1) * P], ident[:])

        def keep(t):
            k, i = divmod(t, PAIR)
            kept[t] = work.tile([P, FEATURES], F32, name="kept")
            nc.vector.tensor_tensor(out=kept[t][:], in0=back[t, FORGET][:], in1=c_sb[k][:, i, :], op=ALU.mult)

        def add_input(t):
            k, i = divmod(t, PAIR)
            if i == 0:
                c_new[k] = stores.tile([P, PAIR, FEATURES], F32, name="c_new")
            nc.gpsimd.tensor_tensor(out=c_new[k][:, i, :], in0=kept[t][:], in1=ic_sb[k][:, i, :], op=ALU.add)

        def squash(t):
            k, i = divmod(t, PAIR)
            squashed[t] = work.tile([P, FEATURES], F32, name="squashed")
            nc.scalar.activation(out=squashed[t][:], in_=c_new[k][:, i, :], func=ACT.Tanh)

        def put_out(t):
            k, i = divmod(t, PAIR)
            if i == 0:
                h_new[k] = stores.tile([P, PAIR, FEATURES], F32, name="h_new")
            nc.vector.tensor_tensor(out=h_new[k][:, i, :], in0=back[t, OUTPUT][:], in1=squashed[t][:], op=ALU.mult)

        def due(step, lag):
            return 0 <= step - lag < ROW_TILES

        for step in range(ROW_TILES + LAG_OUT + 1):
            if step % PAIR == 0:
                if step // PAIR + LOAD_AHEAD < PAIRS:
                    load_x_h(step // PAIR + LOAD_AHEAD, nc.sync)
            if (step - LAG_KEEP) % PAIR == 0:
                if 0 <= (step - LAG_KEEP) // PAIR + LOAD_AHEAD < PAIRS:
                    load_c_ic((step - LAG_KEEP) // PAIR + LOAD_AHEAD)

            if due(step, LAG_KEEP):
                keep(step - LAG_KEEP)
            if due(step, LAG_NORMALISE):
                inverse_deviation(step - LAG_NORMALISE)
            if due(step, LAG_KEEP):
                add_input(step - LAG_KEEP)
            if due(step, LAG_SQUARES):
                negative_mean(step - LAG_SQUARES)
            if due(step, LAG_PRODUCT):
                products(step - LAG_PRODUCT)
            if due(step, LAG_TANH):
                squash(step - LAG_TANH)
            if due(step, LAG_PRODUCT):
                add_bias(step - LAG_PRODUCT)
            if due(step, LAG_BACK_O):
                turn_back(step - LAG_BACK_O, OUTPUT)
            if due(step, LAG_OUT):
                put_out(step - LAG_OUT)
            if due(step, LAG_QUANTISE):
                regroup(step - LAG_QUANTISE)
            if due(step, LAG_SQUARES):
                squares(step - LAG_SQUARES)
            if due(step, 0):
                turn(step)
            if due(step, LAG_GATE):
                turn_normed((step - LAG_GATE) // PAIR, (step - LAG_GATE) % PAIR)
            if due(step, LAG_NORMALISE):
                normalise(step - LAG_NORMALISE)
            if due(step, LAG_GATE):
                sigmoids((step - LAG_GATE) // PAIR, (step - LAG_GATE) % PAIR)
            if due(step, LAG_QUANTISE):
                quantise(step - LAG_QUANTISE)
            if due(step, LAG_SQUARES):
                variance(step - LAG_SQUARES)
            if due(step, LAG_BACK_F):
                turn_back(step - LAG_BACK_F, FORGET)
            if step == CONST_STEP:
                spread_constants()

            if due(step, LAG_KEEP) and (step - LAG_KEEP) % PAIR == PAIR - 1:
                k = (step - LAG_KEEP) // PAIR
                nc.sync.dma_start(out=c_new_rows[:, tiles_of(k), :], in_=c_new[k][:])
            if due(step, LAG_OUT) and (step - LAG_OUT) % PAIR == PAIR - 1:
                k = (step - LAG_OUT) // PAIR
                nc.sync.dma_start(out=h_new_rows[:, tiles_of(k), :], in_=h_new[k][:])
